import numpy as np
import ml_dtypes


def mxq(x, axis, fmt="e4m3"):
    dtype, down = {"e4m3": (ml_dtypes.float8_e4m3fn, 7), "e5m2": (ml_dtypes.float8_e5m2, 14)}[fmt]
    v = np.moveaxis(np.asarray(x, np.float32).astype(ml_dtypes.bfloat16).astype(np.float64), axis, -1)
    blocks = v.reshape(v.shape[:-1] + (-1, 32))
    amax = np.abs(blocks).max(-1, keepdims=True)
    byte = np.maximum(np.where(amax > 0, np.frexp(amax)[1] - 1 + 127, 0) - down, 1)
    scale = np.exp2(byte - 127.0)
    codes = (blocks / scale).astype(np.float32).astype(dtype).astype(np.float64)
    return np.moveaxis((codes * scale).reshape(v.shape), -1, axis)


WIDE = False


def mx_kscale(k):
    if not WIDE:
        return np.ones(k)
    levels = np.array([10, -10, 5, -5, 0])
    if k % 512:
        return np.exp2(np.random.permutation(np.resize(levels, k // 32))).repeat(32)
    a = np.empty((k // 512, 16))
    for p in range(k // 512):
        a[p, :8] = np.random.permutation(np.resize(levels, 8))
        for g in range(8):
            far = levels[np.abs(levels - a[p, g]) >= 10]
            a[p, g + 8] = far[np.random.randint(len(far))]
    return np.exp2(a.ravel()).repeat(32)


BF16 = ml_dtypes.bfloat16


def bf(x):
    return np.asarray(x, np.float32).astype(BF16)


def f64(x):
    return np.asarray(x).astype(np.float64)


B, S, D, H, NOPE, ROPE, VD, KV_RANK, Q_RANK = 2, 2048, 1024, 2, 64, 128, 64, 512, 1536
EPS = 1e-6
THETA = 10000.0
LAT = 0.005
PE = 0.1
HALF = ROPE // 2


def rmsnorm(v, g):
    return v * (1.0 / np.sqrt(np.mean(v * v, axis=-1, keepdims=True) + EPS)) * g


def rope(v):
    inv = 1.0 / THETA ** (np.arange(HALF) / HALF)
    ang = np.arange(S)[:, None] * inv[None, :]
    cos = np.cos(ang)[None, :, None, :]
    sin = np.sin(ang)[None, :, None, :]
    v1, v2 = v[..., :HALF], v[..., HALF:]
    return np.concatenate([v1 * cos - v2 * sin, v2 * cos + v1 * sin], axis=-1)


def setup_inputs():
    s, t = mx_kscale(D), mx_kscale(KV_RANK)
    col = np.concatenate([np.full(KV_RANK, LAT), np.full(ROPE, PE)]) / np.sqrt(D)
    return {"x": bf(np.random.standard_normal((B, S, D)) * s),
            "w_dkv": bf(np.random.standard_normal((D, KV_RANK + ROPE)) * col / s[:, None]),
            "kv_a_norm": bf((1.0 + 0.1 * np.random.standard_normal(KV_RANK)) * t),
            "w_ukv": bf(np.random.standard_normal((KV_RANK, H * (NOPE + VD))) / np.sqrt(KV_RANK) / t[:, None])}


def reference(x, w_dkv, kv_a_norm, w_ukv):
    xq = mxq(f64(x), 2, "e4m3")
    wd = f64(w_dkv)
    c_kv = xq @ mxq(wd[:, :KV_RANK], 0, "e4m3")
    k_pe = xq @ mxq(wd[:, KV_RANK:], 0, "e4m3")
    h = rmsnorm(c_kv, f64(kv_a_norm))
    kv = (mxq(h, 2, "e4m3") @ mxq(f64(w_ukv), 0, "e4m3")).reshape(B, S, H, NOPE + VD)
    k_nope, v = kv[..., :NOPE], kv[..., NOPE:]
    k_pe = rope(k_pe[:, :, None, :])
    kf = np.concatenate([k_nope, np.broadcast_to(k_pe, (B, S, H, ROPE))], axis=-1)
    return kf, v

@@ -1,0 +1,322 @@
+import math
+from contextlib import ExitStack
+
+import concourse.mybir as mybir
+from concourse.masks import make_identity
+
+F32 = mybir.dt.float32
+BF16 = mybir.dt.bfloat16
+I32 = mybir.dt.int32
+U32 = mybir.dt.uint32
+U8 = mybir.dt.uint8
+FP8X4 = mybir.dt.float8_e4m3fn_x4
+ALU = mybir.AluOpType
+ACT = mybir.ActivationFunctionType
+
+P = 128
+PACK = 4
+K_PASS = P * PACK
+
+TOKENS = 2 * 2048
+SEQ = 2048
+D_MODEL = 1024
+LATENT = 512
+ROPE = 128
+HALF = ROPE // 2
+HEADS = 2
+NOPE = 64
+V_DIM = 64
+KV_OUT = HEADS * (NOPE + V_DIM)
+EPS = 1e-6
+THETA = 10000.0
+
+X_PASSES = D_MODEL // K_PASS
+TILES = 2
+ROUND = TILES * P
+ROUNDS = TOKENS // ROUND
+SEQ_ROUNDS = SEQ // ROUND
+
+ROUND_MAGIC = 12582912.0
+
+FLOPS = 2 * TOKENS * D_MODEL * (LATENT + ROPE) + 2 * TOKENS * LATENT * KV_OUT
+
+
+def tile_multiheadlatentattention_pb_t_kernel(tc, x, w_dkv, kv_a_norm, w_ukv, out_0, out_1):
+    nc = tc.nc
+    x_rows = x.flatten_outer_dims()
+    kf_rows = out_0.rearrange("b s h f -> (b s) h f")
+    v_rows = out_1.rearrange("b s h f -> (b s) (h f)")
+
+    with ExitStack() as ctx:
+        keep = ctx.enter_context(tc.tile_pool(name="keep", bufs=1))
+        x_pool = ctx.enter_context(tc.tile_pool(name="x_pool", bufs=ROUNDS))
+        work = ctx.enter_context(tc.tile_pool(name="work", bufs=4))
+        psum_x = ctx.enter_context(tc.psum_pool(name="psum_x", bufs=2))
+        psum_c = ctx.enter_context(tc.psum_pool(name="psum_c", bufs=3))
+        psum_one = ctx.enter_context(tc.psum_pool(name="psum_one", bufs=1))
+        ctx.enter_context(tc.manual_schedule())
+
+        wd_raw = keep.tile([P, X_PASSES, PACK, LATENT + ROPE], BF16)
+        for g in range(X_PASSES):
+            nc.sync.dma_start(
+                out=wd_raw[:, g].rearrange("p t c -> p (t c)"),
+                in_=w_dkv[g * K_PASS : (g + 1) * K_PASS, :].rearrange("(p t) c -> p (t c)", t=PACK),
+            )
+        x_sb = {}
+        for i in range(ROUNDS):
+            x_sb[i] = x_pool.tile([P, TILES * D_MODEL], BF16, name="x_sb")
+            nc.sync.dma_start(
+                out=x_sb[i][:],
+                in_=x_rows[i * ROUND : (i + 1) * ROUND, :].rearrange("(p n) d -> p (n d)", n=TILES),
+            )
+        wu_raw = keep.tile([P, PACK, KV_OUT], BF16)
+        nc.scalar.dma_start(
+            out=wu_raw[:].rearrange("p t n -> p (t n)"),
+            in_=w_ukv.rearrange("(p t) n -> p (t n)", t=PACK),
+        )
+        gain_raw = keep.tile([P, LATENT], BF16)
+        nc.scalar.dma_start(out=gain_raw[:], in_=kv_a_norm.partition_broadcast(P))
+
+        n_pos = SEQ // P
+        pos_int = keep.tile([P, n_pos], I32)
+        nc.gpsimd.iota(pos_int[:], pattern=[[ROUND, SEQ_ROUNDS], [1, TILES]], base=0, channel_multiplier=TILES)
+        identity = keep.tile([P, P], F32)
+        make_identity(nc, identity[:])
+        one = keep.tile([P, 1], F32)
+        nc.vector.memset(one[:], 1.0)
+        freq = keep.tile([P, HALF], F32)
+        nc.vector.tensor_scalar_mul(out=freq[:, 0:1], in0=one[:], scalar1=1.0 / (2.0 * math.pi))
+        filled = 1
+        while filled < HALF:
+            nc.vector.tensor_scalar_mul(
+                out=freq[:, filled : 2 * filled], in0=freq[:, 0:filled], scalar1=THETA ** (-filled / HALF)
+            )
+            filled *= 2
+        pos = keep.tile([P, n_pos], F32)
+        nc.vector.tensor_copy(out=pos[:], in_=pos_int[:])
+        table_shape = [P, n_pos, HALF]
+        turns = keep.tile(table_shape, F32)
+        nc.vector.tensor_tensor(
+            out=turns[:],
+            in0=pos[:].unsqueeze(2).to_broadcast(table_shape),
+            in1=freq[:].unsqueeze(1).to_broadcast(table_shape),
+            op=ALU.mult,
+        )
+        whole = keep.tile(table_shape, F32)
+        nc.vector.tensor_scalar(
+            out=whole[:], in0=turns[:], scalar1=ROUND_MAGIC, scalar2=ROUND_MAGIC, op0=ALU.add, op1=ALU.subtract
+        )
+        frac = keep.tile(table_shape, F32)
+        nc.vector.tensor_tensor(out=frac[:], in0=turns[:], in1=whole[:], op=ALU.subtract)
+        quarter_turn = keep.tile([P, 1], F32)
+        nc.vector.tensor_scalar_mul(out=quarter_turn[:], in0=one[:], scalar1=math.pi / 2.0)
+        eps = keep.tile([P, 1], F32)
+        nc.vector.tensor_scalar_mul(out=eps[:], in0=one[:], scalar1=EPS)
+
+        gain = keep.tile([P, LATENT], BF16)
+        nc.gpsimd.tensor_copy(
+            out=gain[:].rearrange("p (u q e) -> p u q e", u=2, e=2),
+            in_=gain_raw[:].rearrange("p (q u e) -> p u q e", u=2, e=2),
+        )
+        wu_grouped = keep.tile([P, KV_OUT, PACK], BF16, align_bytes=64)
+        nc.scalar.copy(out=wu_grouped[:], in_=wu_raw[:].rearrange("p t n -> p n t"))
+
+        sin_t = keep.tile(table_shape, F32)
+        nc.scalar.activation(out=sin_t[:], in_=frac[:], func=ACT.Sin, scale=2.0 * math.pi)
+        abs_frac = keep.tile(table_shape, F32)
+        nc.scalar.activation(out=abs_frac[:], in_=frac[:], func=ACT.Abs)
+        cos_t = keep.tile(table_shape, F32)
+        nc.scalar.activation(
+            out=cos_t[:], in_=abs_frac[:], func=ACT.Sin, bias=quarter_turn[:], scale=-2.0 * math.pi
+        )
+
+        wd_grouped = keep.tile([P, X_PASSES, LATENT + ROPE, PACK], BF16, align_bytes=64)
+        wd_codes = keep.tile([P, X_PASSES, LATENT + ROPE], U32, align_bytes=64)
+        wd_scales = keep.tile([P, X_PASSES, LATENT + ROPE], U8, align_bytes=64)
+        for g in range(X_PASSES):
+            for u in range(2):
+                nc.vector.tensor_copy(
+                    out=wd_grouped[:, g, 2 * P * u : 2 * P * (u + 1)].rearrange("p (q e) t -> p q t e", e=2),
+                    in_=wd_raw[:, g, :, 0:LATENT].rearrange("p t (q u e) -> p q u t e", u=2, e=2)[:, :, u],
+                )
+            nc.vector.tensor_copy(
+                out=wd_grouped[:, g, LATENT : LATENT + ROPE].rearrange("p (c i) t -> p c t i", i=4),
+                in_=wd_raw[:, g, :, LATENT : LATENT + ROPE].rearrange("p t (c i) -> p c t i", i=4),
+            )
+        for g in range(X_PASSES):
+            for cols in (slice(0, LATENT), slice(LATENT, LATENT + ROPE)):
+                nc.vector.quantize_mx(
+                    out=wd_codes[:, g, cols].bitcast(FP8X4),
+                    scales=wd_scales[:, g, cols],
+                    in_=wd_grouped[:, g, cols, :].rearrange("p c t -> p (c t)"),
+                )
+        wu_codes = keep.tile([P, KV_OUT], U32, align_bytes=64)
+        wu_scales = keep.tile([P, KV_OUT], U8, align_bytes=64)
+        nc.vector.quantize_mx(
+            out=wu_codes[:].bitcast(FP8X4),
+            scales=wu_scales[:],
+            in_=wu_grouped[:].rearrange("p n t -> p (n t)"),
+        )
+
+        x_grouped, x_codes, x_scales = {}, {}, {}
+        latent_ps, key_ps, inv_rms = {}, {}, {}
+        h_sb, h_grouped, h_codes, h_scales = {}, {}, {}, {}
+
+        def transpose_x(i):
+            words = x_sb[i][:].bitcast(F32)
+            n_words = D_MODEL // 2
+            x_grouped[i] = work.tile([P, TILES * n_words], F32, name="x_grouped", align_bytes=64)
+            for n in range(TILES):
+                xt_ps = psum_x.tile([P, 2 * X_PASSES, P], F32, name="xt_ps")
+                for a in range(2 * X_PASSES):
+                    g, u = divmod(a, 2)
+                    start = n * n_words + g * 2 * P
+                    nc.tensor.transpose(xt_ps[:, a, :], words[:, start + u : start + 2 * P : 2], identity[:])
+                copy = nc.scalar.copy if n == 0 else nc.vector.tensor_copy
+                copy(
+                    out=x_grouped[i][:, n * n_words : (n + 1) * n_words].rearrange(
+                        "p (g r u) -> p g r u", g=X_PASSES, u=2
+                    ),
+                    in_=xt_ps[:].rearrange("p (g u) r -> p g r u", u=2),
+                )
+
+        def quantise_x(i):
+            x_codes[i] = work.tile([P, TILES * X_PASSES * P], U32, name="x_codes", align_bytes=64)
+            x_scales[i] = work.tile([P, TILES * X_PASSES * P], U8, name="x_scales", align_bytes=64)
+            nc.vector.quantize_mx(
+                out=x_codes[i][:].bitcast(FP8X4), scales=x_scales[i][:], in_=x_grouped[i][:].bitcast(BF16)
+            )
+
+        def down_project(i):
+            key_ps[i] = psum_one.tile([P, TILES, ROPE], F32, name="key_ps")
+            sum_sq = work.tile([P, TILES], F32, name="sum_sq")
+            for n in range(TILES):
+                latent_ps[i, n] = psum_c.tile([P, LATENT], F32, name="latent_ps")
+                for out, cols in (
+                    (latent_ps[i, n][:], slice(0, LATENT)),
+                    (key_ps[i][:, n, :], slice(LATENT, LATENT + ROPE)),
+                ):
+                    for g in range(X_PASSES):
+                        tokens = slice((n * X_PASSES + g) * P, (n * X_PASSES + g + 1) * P)
+                        nc.tensor.matmul_mx(
+                            out=out,
+                            lhsT=x_codes[i][:, tokens].bitcast(FP8X4),
+                            lhsT_scale=x_scales[i][:, tokens],
+                            rhs=wd_codes[:, g, cols].bitcast(FP8X4),
+                            rhs_scale=wd_scales[:, g, cols],
+                            start=(g == 0),
+                            stop=(g == X_PASSES - 1),
+                        )
+                squares = work.tile([P, LATENT], BF16, name="squares")
+                nc.scalar.activation(
+                    out=squares[:], in_=latent_ps[i, n][:], func=ACT.Square, accum_out=sum_sq[:, n : n + 1]
+                )
+            inv_rms[i] = work.tile([P, TILES], F32, name="inv_rms")
+            nc.scalar.activation(
+                out=inv_rms[i][:], in_=sum_sq[:], func=ACT.Abs_reciprocal_sqrt, bias=eps[:], scale=1.0 / LATENT
+            )
+
+        def rotate_and_store(i):
+            first = (i % SEQ_ROUNDS) * TILES
+            halves = [P, TILES, 2, HALF]
+            key_sb = work.tile(halves, F32, name="key_sb")
+            nc.vector.tensor_copy(out=key_sb[:].rearrange("p n a f -> p n (a f)"), in_=key_ps[i][:])
+            key_cos = work.tile(halves, F32, name="key_cos")
+            nc.gpsimd.tensor_tensor(
+                out=key_cos[:],
+                in0=key_sb[:],
+                in1=cos_t[:, first : first + TILES, :].unsqueeze(2).to_broadcast(halves),
+                op=ALU.mult,
+            )
+            key_sin = work.tile(halves, F32, name="key_sin")
+            nc.gpsimd.tensor_tensor(
+                out=key_sin[:],
+                in0=key_sb[:],
+                in1=sin_t[:, first : first + TILES, :].unsqueeze(2).to_broadcast(halves),
+                op=ALU.mult,
+            )
+            rotated = work.tile(halves, F32, name="rotated")
+            nc.gpsimd.tensor_tensor(
+                out=rotated[:, :, 0, :], in0=key_cos[:, :, 0, :], in1=key_sin[:, :, 1, :], op=ALU.subtract
+            )
+            nc.gpsimd.tensor_tensor(
+                out=rotated[:, :, 1, :], in0=key_cos[:, :, 1, :], in1=key_sin[:, :, 0, :], op=ALU.add
+            )
+            kf = kf_rows[i * ROUND : (i + 1) * ROUND].rearrange("(p n) h f -> p n h f", n=TILES)
+            for head in range(HEADS):
+                nc.sync.dma_start(
+                    out=kf[:, :, head, NOPE : NOPE + ROPE], in_=rotated[:].rearrange("p n a f -> p n (a f)")
+                )
+
+        def normalise(i):
+            h_sb[i] = work.tile([P, TILES * LATENT], BF16, name="h_sb")
+            for n in range(TILES):
+                nc.vector.scalar_tensor_tensor(
+                    out=h_sb[i][:, n * LATENT : (n + 1) * LATENT],
+                    in0=latent_ps[i, n][:],
+                    scalar=inv_rms[i][:, n : n + 1],
+                    in1=gain[:],
+                    op0=ALU.mult,
+                    op1=ALU.mult,
+                )
+
+        def transpose_h(i):
+            words = h_sb[i][:].bitcast(F32)
+            n_words = LATENT // 2
+            ht_ps = psum_one.tile([P, TILES, 2, P], F32, name="ht_ps")
+            for n in range(TILES):
+                for u in range(2):
+                    first = n * n_words + u * P
+                    nc.tensor.transpose(ht_ps[:, n, u, :], words[:, first : first + P], identity[:])
+            h_grouped[i] = work.tile([P, TILES * n_words], F32, name="h_grouped", align_bytes=64)
+            nc.scalar.copy(
+                out=h_grouped[i][:].rearrange("p (n r u) -> p n r u", n=TILES, u=2),
+                in_=ht_ps[:].rearrange("p n u r -> p n r u"),
+            )
+
+        def quantise_h(i):
+            h_codes[i] = work.tile([P, TILES * P], U32, name="h_codes", align_bytes=64)
+            h_scales[i] = work.tile([P, TILES * P], U8, name="h_scales", align_bytes=64)
+            nc.vector.quantize_mx(
+                out=h_codes[i][:].bitcast(FP8X4), scales=h_scales[i][:], in_=h_grouped[i][:].bitcast(BF16)
+            )
+
+        def up_project_and_store(i):
+            kv_ps = psum_one.tile([P, TILES, KV_OUT], F32, name="kv_ps")
+            for n in range(TILES):
+                tokens = slice(n * P, (n + 1) * P)
+                nc.tensor.matmul_mx(
+                    out=kv_ps[:, n, :],
+                    lhsT=h_codes[i][:, tokens].bitcast(FP8X4),
+                    lhsT_scale=h_scales[i][:, tokens],
+                    rhs=wu_codes[:].bitcast(FP8X4),
+                    rhs_scale=wu_scales[:],
+                    start=True,
+                    stop=True,
+                )
+            kv = kv_ps[:].rearrange("p n (h f) -> p n h f", h=HEADS)
+            nope_sb = work.tile([P, TILES, HEADS, NOPE], F32, name="nope_sb")
+            nc.scalar.copy(out=nope_sb[:], in_=kv[:, :, :, 0:NOPE])
+            v_sb = work.tile([P, TILES, HEADS, V_DIM], F32, name="v_sb")
+            nc.scalar.copy(out=v_sb[:], in_=kv[:, :, :, NOPE : NOPE + V_DIM])
+            rows = slice(i * ROUND, (i + 1) * ROUND)
+            kf = kf_rows[rows].rearrange("(p n) h f -> p n h f", n=TILES)
+            nc.sync.dma_start(out=kf[:, :, :, 0:NOPE], in_=nope_sb[:])
+            nc.sync.dma_start(
+                out=v_rows[rows, :].rearrange("(p n) f -> p (n f)", n=TILES),
+                in_=v_sb[:].rearrange("p n h f -> p (n h f)"),
+            )
+
+        def run(stage, i):
+            if 0 <= i < ROUNDS:
+                stage(i)
+
+        for step in range(ROUNDS + 4):
+            run(rotate_and_store, step - 2)
+            run(normalise, step - 2)
+            run(transpose_h, step - 3)
+            run(transpose_x, step)
+            run(quantise_h, step - 3)
+            run(quantise_x, step)
+            run(down_project, step - 1)
+            run(up_project_and_store, step - 4)

@@ -219,19 +219,18 @@ def tile_multiheadlatentattention_pb_t_kernel(tc, x, w_dkv, kv_a_norm, w_ukv, ou
         def rotate_and_store(i):
             first = (i % SEQ_ROUNDS) * TILES
             halves = [P, TILES, 2, HALF]
-            key_sb = work.tile(halves, F32, name="key_sb")
-            nc.vector.tensor_copy(out=key_sb[:].rearrange("p n a f -> p n (a f)"), in_=key_ps[i][:])
+            key = key_ps[i][:].rearrange("p n (a f) -> p n a f", a=2)
             key_cos = work.tile(halves, F32, name="key_cos")
-            nc.gpsimd.tensor_tensor(
+            nc.vector.tensor_tensor(
                 out=key_cos[:],
-                in0=key_sb[:],
+                in0=key,
                 in1=cos_t[:, first : first + TILES, :].unsqueeze(2).to_broadcast(halves),
                 op=ALU.mult,
             )
             key_sin = work.tile(halves, F32, name="key_sin")
-            nc.gpsimd.tensor_tensor(
+            nc.vector.tensor_tensor(
                 out=key_sin[:],
-                in0=key_sb[:],
+                in0=key,
                 in1=sin_t[:, first : first + TILES, :].unsqueeze(2).to_broadcast(halves),
                 op=ALU.mult,
             )

@@ -56,110 +56,141 @@ def tile_multiheadlatentattention_pb_t_kernel(tc, x, w_dkv, kv_a_norm, w_ukv, ou
         psum_one = ctx.enter_context(tc.psum_pool(name="psum_one", bufs=1))
         ctx.enter_context(tc.manual_schedule())
 
+        n_pos = SEQ // P
+        pos = keep.tile([P, n_pos], F32)
+        nc.gpsimd.iota(
+            pos[:],
+            pattern=[[ROUND, SEQ_ROUNDS], [1, TILES]],
+            base=0,
+            channel_multiplier=TILES,
+            allow_small_or_imprecise_dtypes=True,
+        )
+        identity = keep.tile([P, P], F32)
+        make_identity(nc, identity[:])
+
+        x_sb = {}
+
+        def load_x(i):
+            x_sb[i] = x_pool.tile([P, TILES * D_MODEL], BF16, name="x_sb")
+            nc.sync.dma_start(
+                out=x_sb[i][:],
+                in_=x_rows[i * ROUND : (i + 1) * ROUND, :].rearrange("(p n) d -> p (n d)", n=TILES),
+            )
+
+        load_x(0)
         wd_raw = keep.tile([P, X_PASSES, PACK, LATENT + ROPE], BF16)
         for g in range(X_PASSES):
             nc.sync.dma_start(
                 out=wd_raw[:, g].rearrange("p t c -> p (t c)"),
                 in_=w_dkv[g * K_PASS : (g + 1) * K_PASS, :].rearrange("(p t) c -> p (t c)", t=PACK),
             )
-        x_sb = {}
-        for i in range(ROUNDS):
-            x_sb[i] = x_pool.tile([P, TILES * D_MODEL], BF16, name="x_sb")
-            nc.sync.dma_start(
-                out=x_sb[i][:],
-                in_=x_rows[i * ROUND : (i + 1) * ROUND, :].rearrange("(p n) d -> p (n d)", n=TILES),
-            )
+        gain_row = keep.tile([P, LATENT], BF16)
+        nc.gpsimd.memset(gain_row[:].bitcast(I32), 0)
+        ones = keep.tile([P, P], BF16)
+        nc.gpsimd.memset(ones[:], 1.0)
+        nc.sync.dma_start(out=gain_row[0:1, :], in_=kv_a_norm.unsqueeze(0))
+        load_x(1)
         wu_raw = keep.tile([P, PACK, KV_OUT], BF16)
-        nc.scalar.dma_start(
+        nc.sync.dma_start(
             out=wu_raw[:].rearrange("p t n -> p (t n)"),
             in_=w_ukv.rearrange("(p t) n -> p (t n)", t=PACK),
         )
-        gain_raw = keep.tile([P, LATENT], BF16)
-        nc.scalar.dma_start(out=gain_raw[:], in_=kv_a_norm.partition_broadcast(P))
+        for i in range(2, ROUNDS):
+            load_x(i)
 
-        n_pos = SEQ // P
-        pos_int = keep.tile([P, n_pos], I32)
-        nc.gpsimd.iota(pos_int[:], pattern=[[ROUND, SEQ_ROUNDS], [1, TILES]], base=0, channel_multiplier=TILES)
-        identity = keep.tile([P, P], F32)
-        make_identity(nc, identity[:])
-        one = keep.tile([P, 1], F32)
-        nc.vector.memset(one[:], 1.0)
-        freq = keep.tile([P, HALF], F32)
-        nc.vector.tensor_scalar_mul(out=freq[:, 0:1], in0=one[:], scalar1=1.0 / (2.0 * math.pi))
+        table_shape = [P, n_pos, HALF]
+        turns = keep.tile(table_shape, F32)
+        nc.vector.tensor_scalar_mul(out=turns[:, :, 0:1], in0=pos[:].unsqueeze(2), scalar1=1.0 / (2.0 * math.pi))
         filled = 1
         while filled < HALF:
             nc.vector.tensor_scalar_mul(
-                out=freq[:, filled : 2 * filled], in0=freq[:, 0:filled], scalar1=THETA ** (-filled / HALF)
+                out=turns[:, :, filled : 2 * filled], in0=turns[:, :, 0:filled], scalar1=THETA ** (-filled / HALF)
             )
             filled *= 2
-        pos = keep.tile([P, n_pos], F32)
-        nc.vector.tensor_copy(out=pos[:], in_=pos_int[:])
-        table_shape = [P, n_pos, HALF]
-        turns = keep.tile(table_shape, F32)
-        nc.vector.tensor_tensor(
-            out=turns[:],
-            in0=pos[:].unsqueeze(2).to_broadcast(table_shape),
-            in1=freq[:].unsqueeze(1).to_broadcast(table_shape),
-            op=ALU.mult,
-        )
         whole = keep.tile(table_shape, F32)
         nc.vector.tensor_scalar(
             out=whole[:], in0=turns[:], scalar1=ROUND_MAGIC, scalar2=ROUND_MAGIC, op0=ALU.add, op1=ALU.subtract
         )
+        one = keep.tile([P, 1], F32)
+        nc.vector.memset(one[:], 1.0)
         frac = keep.tile(table_shape, F32)
         nc.vector.tensor_tensor(out=frac[:], in0=turns[:], in1=whole[:], op=ALU.subtract)
         quarter_turn = keep.tile([P, 1], F32)
         nc.vector.tensor_scalar_mul(out=quarter_turn[:], in0=one[:], scalar1=math.pi / 2.0)
         eps = keep.tile([P, 1], F32)
         nc.vector.tensor_scalar_mul(out=eps[:], in0=one[:], scalar1=EPS)
-
-        gain = keep.tile([P, LATENT], BF16)
-        nc.gpsimd.tensor_copy(
-            out=gain[:].rearrange("p (u q e) -> p u q e", u=2, e=2),
-            in_=gain_raw[:].rearrange("p (q u e) -> p u q e", u=2, e=2),
-        )
-        wu_grouped = keep.tile([P, KV_OUT, PACK], BF16, align_bytes=64)
-        nc.scalar.copy(out=wu_grouped[:], in_=wu_raw[:].rearrange("p t n -> p n t"))
-
         sin_t = keep.tile(table_shape, F32)
         nc.scalar.activation(out=sin_t[:], in_=frac[:], func=ACT.Sin, scale=2.0 * math.pi)
         abs_frac = keep.tile(table_shape, F32)
-        nc.scalar.activation(out=abs_frac[:], in_=frac[:], func=ACT.Abs)
         cos_t = keep.tile(table_shape, F32)
-        nc.scalar.activation(
-            out=cos_t[:], in_=abs_frac[:], func=ACT.Sin, bias=quarter_turn[:], scale=-2.0 * math.pi
-        )
+
+        def make_cosines():
+            nc.scalar.activation(out=abs_frac[:], in_=frac[:], func=ACT.Abs)
+            nc.scalar.activation(
+                out=cos_t[:], in_=abs_frac[:], func=ACT.Sin, bias=quarter_turn[:], scale=-2.0 * math.pi
+            )
+
+        inv_scratch = keep.tile([P, 1], F32)
+
+        def load_root_table():
+            nc.scalar.activation(out=inv_scratch[:], in_=one[:], func=ACT.Abs_reciprocal_sqrt)
 
         wd_grouped = keep.tile([P, X_PASSES, LATENT + ROPE, PACK], BF16, align_bytes=64)
         wd_codes = keep.tile([P, X_PASSES, LATENT + ROPE], U32, align_bytes=64)
         wd_scales = keep.tile([P, X_PASSES, LATENT + ROPE], U8, align_bytes=64)
-        for g in range(X_PASSES):
+
+        def group_latent_weights(g):
             for u in range(2):
                 nc.vector.tensor_copy(
                     out=wd_grouped[:, g, 2 * P * u : 2 * P * (u + 1)].rearrange("p (q e) t -> p q t e", e=2),
                     in_=wd_raw[:, g, :, 0:LATENT].rearrange("p t (q u e) -> p q u t e", u=2, e=2)[:, :, u],
                 )
+
+        def group_key_weights(g):
             nc.vector.tensor_copy(
                 out=wd_grouped[:, g, LATENT : LATENT + ROPE].rearrange("p (c i) t -> p c t i", i=4),
                 in_=wd_raw[:, g, :, LATENT : LATENT + ROPE].rearrange("p t (c i) -> p c t i", i=4),
             )
-        for g in range(X_PASSES):
-            for cols in (slice(0, LATENT), slice(LATENT, LATENT + ROPE)):
-                nc.vector.quantize_mx(
-                    out=wd_codes[:, g, cols].bitcast(FP8X4),
-                    scales=wd_scales[:, g, cols],
-                    in_=wd_grouped[:, g, cols, :].rearrange("p c t -> p (c t)"),
-                )
+
+        def quantise_weights(g, cols):
+            nc.vector.quantize_mx(
+                out=wd_codes[:, g, cols].bitcast(FP8X4),
+                scales=wd_scales[:, g, cols],
+                in_=wd_grouped[:, g, cols, :].rearrange("p c t -> p (c t)"),
+            )
+
+        LATENT_COLS, KEY_COLS = slice(0, LATENT), slice(LATENT, LATENT + ROPE)
+
+        gain = keep.tile([P, LATENT], BF16)
+
+        gain_ps = psum_one.tile([P, 2 * TILES, P], F32, name="ht_ps")
+
+        def spread_gain():
+            gain_cols = gain_ps[:].rearrange("p n r -> p (n r)")
+            nc.tensor.matmul(gain_cols, lhsT=ones[:], rhs=gain_row[:], start=True, stop=True)
+
+        def copy_gain():
+            nc.vector.tensor_copy(
+                out=gain[:].rearrange("p (u q e) -> p u q e", u=2, e=2),
+                in_=gain_ps[:].rearrange("p n r -> p (n r)").rearrange("p (q u e) -> p u q e", u=2, e=2),
+            )
+
+        wu_grouped = keep.tile([P, KV_OUT, PACK], BF16, align_bytes=64)
         wu_codes = keep.tile([P, KV_OUT], U32, align_bytes=64)
         wu_scales = keep.tile([P, KV_OUT], U8, align_bytes=64)
-        nc.vector.quantize_mx(
-            out=wu_codes[:].bitcast(FP8X4),
-            scales=wu_scales[:],
-            in_=wu_grouped[:].rearrange("p n t -> p (n t)"),
-        )
+
+        def group_up_weights():
+            nc.scalar.copy(out=wu_grouped[:], in_=wu_raw[:].rearrange("p t n -> p n t"))
+
+        def quantise_up_weights():
+            nc.vector.quantize_mx(
+                out=wu_codes[:].bitcast(FP8X4),
+                scales=wu_scales[:],
+                in_=wu_grouped[:].rearrange("p n t -> p (n t)"),
+            )
 
         x_grouped, x_codes, x_scales = {}, {}, {}
-        latent_ps, key_ps, inv_rms = {}, {}, {}
+        latent_ps, key_ps, sum_sq, inv_rms = {}, {}, {}, {}
         h_sb, h_grouped, h_codes, h_scales = {}, {}, {}, {}
 
         def transpose_x(i):
@@ -187,33 +218,36 @@ def tile_multiheadlatentattention_pb_t_kernel(tc, x, w_dkv, kv_a_norm, w_ukv, ou
                 out=x_codes[i][:].bitcast(FP8X4), scales=x_scales[i][:], in_=x_grouped[i][:].bitcast(BF16)
             )
 
-        def down_project(i):
-            key_ps[i] = psum_one.tile([P, TILES, ROPE], F32, name="key_ps")
-            sum_sq = work.tile([P, TILES], F32, name="sum_sq")
-            for n in range(TILES):
-                latent_ps[i, n] = psum_c.tile([P, LATENT], F32, name="latent_ps")
-                for out, cols in (
-                    (latent_ps[i, n][:], slice(0, LATENT)),
-                    (key_ps[i][:, n, :], slice(LATENT, LATENT + ROPE)),
-                ):
-                    for g in range(X_PASSES):
-                        tokens = slice((n * X_PASSES + g) * P, (n * X_PASSES + g + 1) * P)
-                        nc.tensor.matmul_mx(
-                            out=out,
-                            lhsT=x_codes[i][:, tokens].bitcast(FP8X4),
-                            lhsT_scale=x_scales[i][:, tokens],
-                            rhs=wd_codes[:, g, cols].bitcast(FP8X4),
-                            rhs_scale=wd_scales[:, g, cols],
-                            start=(g == 0),
-                            stop=(g == X_PASSES - 1),
-                        )
-                squares = work.tile([P, LATENT], BF16, name="squares")
-                nc.scalar.activation(
-                    out=squares[:], in_=latent_ps[i, n][:], func=ACT.Square, accum_out=sum_sq[:, n : n + 1]
-                )
-            inv_rms[i] = work.tile([P, TILES], F32, name="inv_rms")
+        def down_project(i, n):
+            if n == 0:
+                key_ps[i] = psum_one.tile([P, TILES, ROPE], F32, name="key_ps")
+                sum_sq[i] = work.tile([P, TILES], F32, name="sum_sq")
+                inv_rms[i] = work.tile([P, TILES], F32, name="inv_rms")
+            latent_ps[i, n] = psum_c.tile([P, LATENT], F32, name="latent_ps")
+            for out, cols in ((latent_ps[i, n][:], LATENT_COLS), (key_ps[i][:, n, :], KEY_COLS)):
+                for g in range(X_PASSES):
+                    tokens = slice((n * X_PASSES + g) * P, (n * X_PASSES + g + 1) * P)
+                    nc.tensor.matmul_mx(
+                        out=out,
+                        lhsT=x_codes[i][:, tokens].bitcast(FP8X4),
+                        lhsT_scale=x_scales[i][:, tokens],
+                        rhs=wd_codes[:, g, cols].bitcast(FP8X4),
+                        rhs_scale=wd_scales[:, g, cols],
+                        start=(g == 0),
+                        stop=(g == X_PASSES - 1),
+                    )
+            squares = work.tile([P, LATENT], BF16, name="squares")
             nc.scalar.activation(
-                out=inv_rms[i][:], in_=sum_sq[:], func=ACT.Abs_reciprocal_sqrt, bias=eps[:], scale=1.0 / LATENT
+                out=squares[:], in_=latent_ps[i, n][:], func=ACT.Square, accum_out=sum_sq[i][:, n : n + 1]
+            )
+
+        def invert_rms(i, tiles):
+            nc.scalar.activation(
+                out=inv_rms[i][:, tiles],
+                in_=sum_sq[i][:, tiles],
+                func=ACT.Abs_reciprocal_sqrt,
+                bias=eps[:],
+                scale=1.0 / LATENT,
             )
 
         def rotate_and_store(i):
@@ -247,75 +281,120 @@ def tile_multiheadlatentattention_pb_t_kernel(tc, x, w_dkv, kv_a_norm, w_ukv, ou
                     out=kf[:, :, head, NOPE : NOPE + ROPE], in_=rotated[:].rearrange("p n a f -> p n (a f)")
                 )
 
-        def normalise(i):
-            h_sb[i] = work.tile([P, TILES * LATENT], BF16, name="h_sb")
-            for n in range(TILES):
-                nc.vector.scalar_tensor_tensor(
-                    out=h_sb[i][:, n * LATENT : (n + 1) * LATENT],
-                    in0=latent_ps[i, n][:],
-                    scalar=inv_rms[i][:, n : n + 1],
-                    in1=gain[:],
-                    op0=ALU.mult,
-                    op1=ALU.mult,
-                )
+        def normalise(i, n):
+            if n == 0:
+                h_sb[i] = work.tile([P, TILES, LATENT], BF16, name="h_sb")
+            nc.vector.scalar_tensor_tensor(
+                out=h_sb[i][:, n, :],
+                in0=latent_ps[i, n][:],
+                scalar=inv_rms[i][:, n : n + 1],
+                in1=gain[:],
+                op0=ALU.mult,
+                op1=ALU.mult,
+            )
 
-        def transpose_h(i):
-            words = h_sb[i][:].bitcast(F32)
-            n_words = LATENT // 2
-            ht_ps = psum_one.tile([P, TILES, 2, P], F32, name="ht_ps")
-            for n in range(TILES):
+        def transpose_h(i, tiles, ht_ps, copy):
+            if tiles.start == 0:
+                h_grouped[i] = work.tile([P, TILES, 2 * P], F32, name="h_grouped", align_bytes=64)
+            for j, n in enumerate(range(tiles.start, tiles.stop)):
+                words = h_sb[i][:, n, :].bitcast(F32)
                 for u in range(2):
-                    first = n * n_words + u * P
-                    nc.tensor.transpose(ht_ps[:, n, u, :], words[:, first : first + P], identity[:])
-            h_grouped[i] = work.tile([P, TILES * n_words], F32, name="h_grouped", align_bytes=64)
-            nc.scalar.copy(
-                out=h_grouped[i][:].rearrange("p (n r u) -> p n r u", n=TILES, u=2),
-                in_=ht_ps[:].rearrange("p n u r -> p n r u"),
+                    nc.tensor.transpose(ht_ps[:, 2 * j + u, :], words[:, u * P : (u + 1) * P], identity[:])
+            copy(
+                out=h_grouped[i][:, tiles, :].rearrange("p n (r u) -> p n r u", u=2),
+                in_=ht_ps[:, 0 : 2 * (tiles.stop - tiles.start), :].rearrange("p (n u) r -> p n r u", u=2),
             )
 
-        def quantise_h(i):
-            h_codes[i] = work.tile([P, TILES * P], U32, name="h_codes", align_bytes=64)
-            h_scales[i] = work.tile([P, TILES * P], U8, name="h_scales", align_bytes=64)
+        def quantise_h(i, tiles):
+            if tiles.start == 0:
+                h_codes[i] = work.tile([P, TILES, P], U32, name="h_codes", align_bytes=64)
+                h_scales[i] = work.tile([P, TILES, P], U8, name="h_scales", align_bytes=64)
             nc.vector.quantize_mx(
-                out=h_codes[i][:].bitcast(FP8X4), scales=h_scales[i][:], in_=h_grouped[i][:].bitcast(BF16)
+                out=h_codes[i][:, tiles, :].rearrange("p n r -> p (n r)").bitcast(FP8X4),
+                scales=h_scales[i][:, tiles, :].rearrange("p n r -> p (n r)"),
+                in_=h_grouped[i][:, tiles, :].rearrange("p n w -> p (n w)").bitcast(BF16),
             )
 
-        def up_project_and_store(i):
-            kv_ps = psum_one.tile([P, TILES, KV_OUT], F32, name="kv_ps")
-            for n in range(TILES):
-                tokens = slice(n * P, (n + 1) * P)
+        def up_project_and_store(i, tiles, kv_ps, copy):
+            count = tiles.stop - tiles.start
+            for j, n in enumerate(range(tiles.start, tiles.stop)):
                 nc.tensor.matmul_mx(
-                    out=kv_ps[:, n, :],
-                    lhsT=h_codes[i][:, tokens].bitcast(FP8X4),
-                    lhsT_scale=h_scales[i][:, tokens],
+                    out=kv_ps[:, j * KV_OUT : (j + 1) * KV_OUT],
+                    lhsT=h_codes[i][:, n, :].bitcast(FP8X4),
+                    lhsT_scale=h_scales[i][:, n, :],
                     rhs=wu_codes[:].bitcast(FP8X4),
                     rhs_scale=wu_scales[:],
                     start=True,
                     stop=True,
                 )
-            kv = kv_ps[:].rearrange("p n (h f) -> p n h f", h=HEADS)
-            nope_sb = work.tile([P, TILES, HEADS, NOPE], F32, name="nope_sb")
-            nc.scalar.copy(out=nope_sb[:], in_=kv[:, :, :, 0:NOPE])
-            v_sb = work.tile([P, TILES, HEADS, V_DIM], F32, name="v_sb")
-            nc.scalar.copy(out=v_sb[:], in_=kv[:, :, :, NOPE : NOPE + V_DIM])
+            kv_sb = work.tile([P, 2, count, HEADS, NOPE], F32, name="kv_sb")
+            copy(
+                out=kv_sb[:].rearrange("p a n h f -> p (n h) a f"),
+                in_=kv_ps[:, 0 : count * KV_OUT].rearrange("p (m a f) -> p m a f", a=2, f=NOPE),
+            )
             rows = slice(i * ROUND, (i + 1) * ROUND)
             kf = kf_rows[rows].rearrange("(p n) h f -> p n h f", n=TILES)
-            nc.sync.dma_start(out=kf[:, :, :, 0:NOPE], in_=nope_sb[:])
-            nc.sync.dma_start(
-                out=v_rows[rows, :].rearrange("(p n) f -> p (n f)", n=TILES),
-                in_=v_sb[:].rearrange("p n h f -> p (n h f)"),
-            )
+            nc.sync.dma_start(out=kf[:, tiles, :, 0:NOPE], in_=kv_sb[:, 0])
+            v = v_rows[rows].rearrange("(p n) f -> p n f", n=TILES)
+            nc.sync.dma_start(out=v[:, tiles, :], in_=kv_sb[:, 1].rearrange("p n h f -> p n (h f)"))
 
-        def run(stage, i):
-            if 0 <= i < ROUNDS:
-                stage(i)
+        BOTH, FIRST, SECOND = slice(0, 2), slice(0, 1), slice(1, 2)
 
-        for step in range(ROUNDS + 4):
-            run(rotate_and_store, step - 2)
-            run(normalise, step - 2)
-            run(transpose_h, step - 3)
-            run(transpose_x, step)
-            run(quantise_h, step - 3)
-            run(quantise_x, step)
-            run(down_project, step - 1)
-            run(up_project_and_store, step - 4)
+        group_latent_weights(0)
+        transpose_x(0)
+        spread_gain()
+        quantise_weights(0, LATENT_COLS)
+        make_cosines()
+        group_latent_weights(1)
+        quantise_x(0)
+        quantise_weights(1, LATENT_COLS)
+        for g in range(X_PASSES):
+            group_key_weights(g)
+        for g in range(X_PASSES):
+            quantise_weights(g, KEY_COLS)
+        copy_gain()
+
+        LAST = ROUNDS - 1
+        for step in range(1, ROUNDS + 2):
+            r_x, r_c, r_h, r_t, r_kv = step, step - 1, step - 2, step - 3, step - 4
+            if 0 <= r_h < LAST:
+                rotate_and_store(r_h)
+                for n in range(TILES):
+                    normalise(r_h, n)
+            elif r_h == LAST:
+                for n in range(TILES):
+                    normalise(LAST, n)
+                rotate_and_store(LAST)
+            if 0 <= r_t < LAST:
+                transpose_h(r_t, BOTH, psum_one.tile([P, 2 * TILES, P], F32, name="ht_ps"), nc.scalar.copy)
+            if r_x < ROUNDS:
+                transpose_x(r_x)
+            if 0 <= r_t < LAST:
+                quantise_h(r_t, BOTH)
+            if r_x < ROUNDS:
+                quantise_x(r_x)
+            if step == 1:
+                load_root_table()
+            if step == 2:
+                group_up_weights()
+            if step == 3:
+                quantise_up_weights()
+            if 0 <= r_c < LAST:
+                for n in range(TILES):
+                    down_project(r_c, n)
+                invert_rms(r_c, BOTH)
+            elif r_c == LAST:
+                for n, tile in enumerate((FIRST, SECOND)):
+                    down_project(LAST, n)
+                    invert_rms(LAST, tile)
+            if 0 <= r_kv:
+                copy = nc.vector.tensor_copy if step == ROUNDS else nc.scalar.copy
+                up_project_and_store(r_kv, BOTH, psum_one.tile([P, TILES * KV_OUT], F32, name="kv_ps"), copy)
+
+        transpose_h(LAST, FIRST, psum_one.tile([P, 2 * TILES, P], F32, name="ht_ps"), nc.scalar.copy)
+        quantise_h(LAST, FIRST)
+        transpose_h(LAST, SECOND, psum_x.tile([P, 2 * X_PASSES, P], F32, name="xt_ps"), nc.vector.tensor_copy)
+        quantise_h(LAST, SECOND)
+        up_project_and_store(LAST - 1, BOTH, psum_one.tile([P, TILES * KV_OUT], F32, name="kv_ps"), nc.vector.tensor_copy)
+        up_project_and_store(LAST, FIRST, psum_c.tile([P, LATENT], F32, name="latent_ps"), nc.scalar.copy)
+        up_project_and_store(LAST, SECOND, psum_c.tile([P, LATENT], F32, name="latent_ps"), nc.vector.tensor_copy)

@@ -103,31 +103,41 @@ def tile_multiheadlatentattention_pb_t_kernel(tc, x, w_dkv, kv_a_norm, w_ukv, ou
         nc.vector.tensor_scalar_mul(out=turns[:, :, 0:1], in0=pos[:].unsqueeze(2), scalar1=1.0 / (2.0 * math.pi))
         filled = 1
         while filled < HALF:
-            nc.vector.tensor_scalar_mul(
-                out=turns[:, :, filled : 2 * filled], in0=turns[:, :, 0:filled], scalar1=THETA ** (-filled / HALF)
-            )
-            filled *= 2
-        whole = keep.tile(table_shape, F32)
+            for part in range(1, 4):
+                nc.vector.tensor_scalar_mul(
+                    out=turns[:, :, part * filled : (part + 1) * filled],
+                    in0=turns[:, :, 0:filled],
+                    scalar1=THETA ** (-part * filled / HALF),
+                )
+            filled *= 4
+        fast = sum(1 for i in range(HALF) if SEQ * THETA ** (-i / HALF) > math.pi)
+        whole = keep.tile([P, n_pos, fast], F32)
         nc.vector.tensor_scalar(
-            out=whole[:], in0=turns[:], scalar1=ROUND_MAGIC, scalar2=ROUND_MAGIC, op0=ALU.add, op1=ALU.subtract
+            out=whole[:],
+            in0=turns[:, :, 0:fast],
+            scalar1=ROUND_MAGIC,
+            scalar2=ROUND_MAGIC,
+            op0=ALU.add,
+            op1=ALU.subtract,
         )
-        one = keep.tile([P, 1], F32)
-        nc.vector.memset(one[:], 1.0)
-        frac = keep.tile(table_shape, F32)
-        nc.vector.tensor_tensor(out=frac[:], in0=turns[:], in1=whole[:], op=ALU.subtract)
-        quarter_turn = keep.tile([P, 1], F32)
-        nc.vector.tensor_scalar_mul(out=quarter_turn[:], in0=one[:], scalar1=math.pi / 2.0)
-        eps = keep.tile([P, 1], F32)
-        nc.vector.tensor_scalar_mul(out=eps[:], in0=one[:], scalar1=EPS)
+        nc.vector.tensor_tensor(
+            out=turns[:, :, 0:fast], in0=turns[:, :, 0:fast], in1=whole[:], op=ALU.subtract
+        )
         sin_t = keep.tile(table_shape, F32)
-        nc.scalar.activation(out=sin_t[:], in_=frac[:], func=ACT.Sin, scale=2.0 * math.pi)
-        abs_frac = keep.tile(table_shape, F32)
+        nc.scalar.activation(out=sin_t[:], in_=turns[:], func=ACT.Sin, scale=2.0 * math.pi)
+        one = keep.tile([P, 1], F32)
+        nc.gpsimd.memset(one[:], 1.0)
+        quarter_turn = keep.tile([P, 1], F32)
+        nc.gpsimd.tensor_scalar_mul(out=quarter_turn[:], in0=one[:], scalar1=math.pi / 2.0)
+        eps = keep.tile([P, 1], F32)
+        nc.gpsimd.tensor_scalar_mul(out=eps[:], in0=one[:], scalar1=EPS)
+        abs_turns = keep.tile(table_shape, F32)
         cos_t = keep.tile(table_shape, F32)
 
         def make_cosines():
-            nc.scalar.activation(out=abs_frac[:], in_=frac[:], func=ACT.Abs)
+            nc.scalar.activation(out=abs_turns[:], in_=turns[:], func=ACT.Abs)
             nc.scalar.activation(
-                out=cos_t[:], in_=abs_frac[:], func=ACT.Sin, bias=quarter_turn[:], scale=-2.0 * math.pi
+                out=cos_t[:], in_=abs_turns[:], func=ACT.Sin, bias=quarter_turn[:], scale=-2.0 * math.pi
             )
 
         inv_scratch = keep.tile([P, 1], F32)
@@ -203,7 +213,7 @@ def tile_multiheadlatentattention_pb_t_kernel(tc, x, w_dkv, kv_a_norm, w_ukv, ou
                     g, u = divmod(a, 2)
                     start = n * n_words + g * 2 * P
                     nc.tensor.transpose(xt_ps[:, a, :], words[:, start + u : start + 2 * P : 2], identity[:])
-                copy = nc.scalar.copy if n == 0 else nc.vector.tensor_copy
+                copy = nc.scalar.copy if n == 0 or i % 4 == 0 else nc.vector.tensor_copy
                 copy(
                     out=x_grouped[i][:, n * n_words : (n + 1) * n_words].rearrange(
                         "p (g r u) -> p g r u", g=X_PASSES, u=2
@@ -384,17 +394,20 @@ def tile_multiheadlatentattention_pb_t_kernel(tc, x, w_dkv, kv_a_norm, w_ukv, ou
                     down_project(r_c, n)
                 invert_rms(r_c, BOTH)
             elif r_c == LAST:
-                for n, tile in enumerate((FIRST, SECOND)):
-                    down_project(LAST, n)
-                    invert_rms(LAST, tile)
-            if 0 <= r_kv:
-                copy = nc.vector.tensor_copy if step == ROUNDS else nc.scalar.copy
-                up_project_and_store(r_kv, BOTH, psum_one.tile([P, TILES * KV_OUT], F32, name="kv_ps"), copy)
+                down_project(LAST, 0)
+                invert_rms(LAST, FIRST)
+                up_project_and_store(
+                    r_kv, BOTH, psum_one.tile([P, TILES * KV_OUT], F32, name="kv_ps"), nc.vector.tensor_copy
+                )
+                down_project(LAST, 1)
+                invert_rms(LAST, SECOND)
+            if 0 <= r_kv and step != ROUNDS:
+                up_project_and_store(r_kv, BOTH, psum_one.tile([P, TILES * KV_OUT], F32, name="kv_ps"), nc.scalar.copy)
 
         transpose_h(LAST, FIRST, psum_one.tile([P, 2 * TILES, P], F32, name="ht_ps"), nc.scalar.copy)
         quantise_h(LAST, FIRST)
         transpose_h(LAST, SECOND, psum_x.tile([P, 2 * X_PASSES, P], F32, name="xt_ps"), nc.vector.tensor_copy)
         quantise_h(LAST, SECOND)
-        up_project_and_store(LAST - 1, BOTH, psum_one.tile([P, TILES * KV_OUT], F32, name="kv_ps"), nc.vector.tensor_copy)
+        up_project_and_store(LAST - 1, BOTH, psum_one.tile([P, TILES * KV_OUT], F32, name="kv_ps"), nc.scalar.copy)
         up_project_and_store(LAST, FIRST, psum_c.tile([P, LATENT], F32, name="latent_ps"), nc.scalar.copy)
         up_project_and_store(LAST, SECOND, psum_c.tile([P, LATENT], F32, name="latent_ps"), nc.vector.tensor_copy)

@@ -77,13 +77,17 @@ def tile_multiheadlatentattention_pb_t_kernel(tc, x, w_dkv, kv_a_norm, w_ukv, ou
                 in_=x_rows[i * ROUND : (i + 1) * ROUND, :].rearrange("(p n) d -> p (n d)", n=TILES),
             )
 
-        load_x(0)
         wd_raw = keep.tile([P, X_PASSES, PACK, LATENT + ROPE], BF16)
-        for g in range(X_PASSES):
+
+        def load_down_weights(g):
             nc.sync.dma_start(
                 out=wd_raw[:, g].rearrange("p t c -> p (t c)"),
                 in_=w_dkv[g * K_PASS : (g + 1) * K_PASS, :].rearrange("(p t) c -> p (t c)", t=PACK),
             )
+
+        load_x(0)
+        for g in range(X_PASSES):
+            load_down_weights(g)
         gain_row = keep.tile([P, LATENT], BF16)
         nc.gpsimd.memset(gain_row[:].bitcast(I32), 0)
         ones = keep.tile([P, P], BF16)
@@ -123,8 +127,8 @@ def tile_multiheadlatentattention_pb_t_kernel(tc, x, w_dkv, kv_a_norm, w_ukv, ou
         nc.vector.tensor_tensor(
             out=turns[:, :, 0:fast], in0=turns[:, :, 0:fast], in1=whole[:], op=ALU.subtract
         )
-        sin_t = keep.tile(table_shape, F32)
-        nc.scalar.activation(out=sin_t[:], in_=turns[:], func=ACT.Sin, scale=2.0 * math.pi)
+        trig = keep.tile([P, n_pos, 2, HALF], F32)
+        nc.scalar.activation(out=trig[:, :, 1, :], in_=turns[:], func=ACT.Sin, scale=2.0 * math.pi)
         one = keep.tile([P, 1], F32)
         nc.gpsimd.memset(one[:], 1.0)
         quarter_turn = keep.tile([P, 1], F32)
@@ -132,12 +136,11 @@ def tile_multiheadlatentattention_pb_t_kernel(tc, x, w_dkv, kv_a_norm, w_ukv, ou
         eps = keep.tile([P, 1], F32)
         nc.gpsimd.tensor_scalar_mul(out=eps[:], in0=one[:], scalar1=EPS)
         abs_turns = keep.tile(table_shape, F32)
-        cos_t = keep.tile(table_shape, F32)
 
         def make_cosines():
             nc.scalar.activation(out=abs_turns[:], in_=turns[:], func=ACT.Abs)
             nc.scalar.activation(
-                out=cos_t[:], in_=abs_turns[:], func=ACT.Sin, bias=quarter_turn[:], scale=-2.0 * math.pi
+                out=trig[:, :, 0, :], in_=abs_turns[:], func=ACT.Sin, bias=quarter_turn[:], scale=-2.0 * math.pi
             )
 
         inv_scratch = keep.tile([P, 1], F32)
@@ -213,7 +216,7 @@ def tile_multiheadlatentattention_pb_t_kernel(tc, x, w_dkv, kv_a_norm, w_ukv, ou
                     g, u = divmod(a, 2)
                     start = n * n_words + g * 2 * P
                     nc.tensor.transpose(xt_ps[:, a, :], words[:, start + u : start + 2 * P : 2], identity[:])
-                copy = nc.scalar.copy if n == 0 or i % 4 == 0 else nc.vector.tensor_copy
+                copy = nc.scalar.copy if (n == 0 and i != 1) or i % 4 == 0 else nc.vector.tensor_copy
                 copy(
                     out=x_grouped[i][:, n * n_words : (n + 1) * n_words].rearrange(
                         "p (g r u) -> p g r u", g=X_PASSES, u=2
@@ -228,28 +231,34 @@ def tile_multiheadlatentattention_pb_t_kernel(tc, x, w_dkv, kv_a_norm, w_ukv, ou
                 out=x_codes[i][:].bitcast(FP8X4), scales=x_scales[i][:], in_=x_grouped[i][:].bitcast(BF16)
             )
 
-        def down_project(i, n):
+        def multiply_down(out, i, n, cols):
+            for g in range(X_PASSES):
+                tokens = slice((n * X_PASSES + g) * P, (n * X_PASSES + g + 1) * P)
+                nc.tensor.matmul_mx(
+                    out=out,
+                    lhsT=x_codes[i][:, tokens].bitcast(FP8X4),
+                    lhsT_scale=x_scales[i][:, tokens],
+                    rhs=wd_codes[:, g, cols].bitcast(FP8X4),
+                    rhs_scale=wd_scales[:, g, cols],
+                    start=(g == 0),
+                    stop=(g == X_PASSES - 1),
+                )
+
+        def project_latent(i, n):
             if n == 0:
-                key_ps[i] = psum_one.tile([P, TILES, ROPE], F32, name="key_ps")
                 sum_sq[i] = work.tile([P, TILES], F32, name="sum_sq")
                 inv_rms[i] = work.tile([P, TILES], F32, name="inv_rms")
             latent_ps[i, n] = psum_c.tile([P, LATENT], F32, name="latent_ps")
-            for out, cols in ((latent_ps[i, n][:], LATENT_COLS), (key_ps[i][:, n, :], KEY_COLS)):
-                for g in range(X_PASSES):
-                    tokens = slice((n * X_PASSES + g) * P, (n * X_PASSES + g + 1) * P)
-                    nc.tensor.matmul_mx(
-                        out=out,
-                        lhsT=x_codes[i][:, tokens].bitcast(FP8X4),
-                        lhsT_scale=x_scales[i][:, tokens],
-                        rhs=wd_codes[:, g, cols].bitcast(FP8X4),
-                        rhs_scale=wd_scales[:, g, cols],
-                        start=(g == 0),
-                        stop=(g == X_PASSES - 1),
-                    )
+            multiply_down(latent_ps[i, n][:], i, n, LATENT_COLS)
             squares = work.tile([P, LATENT], BF16, name="squares")
             nc.scalar.activation(
                 out=squares[:], in_=latent_ps[i, n][:], func=ACT.Square, accum_out=sum_sq[i][:, n : n + 1]
             )
+
+        def project_key(i):
+            key_ps[i] = psum_one.tile([P, TILES, ROPE], F32, name="key_ps")
+            for n in range(TILES):
+                multiply_down(key_ps[i][:, n, :], i, n, KEY_COLS)
 
         def invert_rms(i, tiles):
             nc.scalar.activation(
@@ -262,28 +271,20 @@ def tile_multiheadlatentattention_pb_t_kernel(tc, x, w_dkv, kv_a_norm, w_ukv, ou
 
         def rotate_and_store(i):
             first = (i % SEQ_ROUNDS) * TILES
-            halves = [P, TILES, 2, HALF]
-            key = key_ps[i][:].rearrange("p n (a f) -> p n a f", a=2)
-            key_cos = work.tile(halves, F32, name="key_cos")
+            shape = [P, TILES, 2, 2, HALF]
+            products = work.tile(shape, F32, name="products")
             nc.vector.tensor_tensor(
-                out=key_cos[:],
-                in0=key,
-                in1=cos_t[:, first : first + TILES, :].unsqueeze(2).to_broadcast(halves),
+                out=products[:],
+                in0=key_ps[i][:].rearrange("p n (a f) -> p n a f", a=2).unsqueeze(2).to_broadcast(shape),
+                in1=trig[:, first : first + TILES].unsqueeze(3).to_broadcast(shape),
                 op=ALU.mult,
             )
-            key_sin = work.tile(halves, F32, name="key_sin")
-            nc.vector.tensor_tensor(
-                out=key_sin[:],
-                in0=key,
-                in1=sin_t[:, first : first + TILES, :].unsqueeze(2).to_broadcast(halves),
-                op=ALU.mult,
-            )
-            rotated = work.tile(halves, F32, name="rotated")
+            rotated = work.tile([P, TILES, 2, HALF], F32, name="rotated")
             nc.gpsimd.tensor_tensor(
-                out=rotated[:, :, 0, :], in0=key_cos[:, :, 0, :], in1=key_sin[:, :, 1, :], op=ALU.subtract
+                out=rotated[:, :, 0, :], in0=products[:, :, 0, 0, :], in1=products[:, :, 1, 1, :], op=ALU.subtract
             )
             nc.gpsimd.tensor_tensor(
-                out=rotated[:, :, 1, :], in0=key_cos[:, :, 1, :], in1=key_sin[:, :, 0, :], op=ALU.add
+                out=rotated[:, :, 1, :], in0=products[:, :, 0, 1, :], in1=products[:, :, 1, 0, :], op=ALU.add
             )
             kf = kf_rows[i * ROUND : (i + 1) * ROUND].rearrange("(p n) h f -> p n h f", n=TILES)
             for head in range(HEADS):
@@ -325,7 +326,7 @@ def tile_multiheadlatentattention_pb_t_kernel(tc, x, w_dkv, kv_a_norm, w_ukv, ou
                 in_=h_grouped[i][:, tiles, :].rearrange("p n w -> p (n w)").bitcast(BF16),
             )
 
-        def up_project_and_store(i, tiles, kv_ps, copy):
+        def up_project_and_store(i, tiles, kv_ps, copy, queue=nc.sync):
             count = tiles.stop - tiles.start
             for j, n in enumerate(range(tiles.start, tiles.stop)):
                 nc.tensor.matmul_mx(
@@ -344,9 +345,9 @@ def tile_multiheadlatentattention_pb_t_kernel(tc, x, w_dkv, kv_a_norm, w_ukv, ou
             )
             rows = slice(i * ROUND, (i + 1) * ROUND)
             kf = kf_rows[rows].rearrange("(p n) h f -> p n h f", n=TILES)
-            nc.sync.dma_start(out=kf[:, tiles, :, 0:NOPE], in_=kv_sb[:, 0])
+            queue.dma_start(out=kf[:, tiles, :, 0:NOPE], in_=kv_sb[:, 0])
             v = v_rows[rows].rearrange("(p n) f -> p n f", n=TILES)
-            nc.sync.dma_start(out=v[:, tiles, :], in_=kv_sb[:, 1].rearrange("p n h f -> p n (h f)"))
+            queue.dma_start(out=v[:, tiles, :], in_=kv_sb[:, 1].rearrange("p n h f -> p n (h f)"))
 
         BOTH, FIRST, SECOND = slice(0, 2), slice(0, 1), slice(1, 2)
 
@@ -355,6 +356,7 @@ def tile_multiheadlatentattention_pb_t_kernel(tc, x, w_dkv, kv_a_norm, w_ukv, ou
         spread_gain()
         quantise_weights(0, LATENT_COLS)
         make_cosines()
+        load_root_table()
         group_latent_weights(1)
         quantise_x(0)
         quantise_weights(1, LATENT_COLS)
@@ -383,24 +385,24 @@ def tile_multiheadlatentattention_pb_t_kernel(tc, x, w_dkv, kv_a_norm, w_ukv, ou
                 quantise_h(r_t, BOTH)
             if r_x < ROUNDS:
                 quantise_x(r_x)
-            if step == 1:
-                load_root_table()
             if step == 2:
                 group_up_weights()
             if step == 3:
                 quantise_up_weights()
             if 0 <= r_c < LAST:
                 for n in range(TILES):
-                    down_project(r_c, n)
+                    project_latent(r_c, n)
                 invert_rms(r_c, BOTH)
+                project_key(r_c)
             elif r_c == LAST:
-                down_project(LAST, 0)
+                project_latent(LAST, 0)
                 invert_rms(LAST, FIRST)
                 up_project_and_store(
                     r_kv, BOTH, psum_one.tile([P, TILES * KV_OUT], F32, name="kv_ps"), nc.vector.tensor_copy
                 )
-                down_project(LAST, 1)
+                project_latent(LAST, 1)
                 invert_rms(LAST, SECOND)
+                project_key(LAST)
             if 0 <= r_kv and step != ROUNDS:
                 up_project_and_store(r_kv, BOTH, psum_one.tile([P, TILES * KV_OUT], F32, name="kv_ps"), nc.scalar.copy)
 
@@ -408,6 +410,7 @@ def tile_multiheadlatentattention_pb_t_kernel(tc, x, w_dkv, kv_a_norm, w_ukv, ou
         quantise_h(LAST, FIRST)
         transpose_h(LAST, SECOND, psum_x.tile([P, 2 * X_PASSES, P], F32, name="xt_ps"), nc.vector.tensor_copy)
         quantise_h(LAST, SECOND)
-        up_project_and_store(LAST - 1, BOTH, psum_one.tile([P, TILES * KV_OUT], F32, name="kv_ps"), nc.scalar.copy)
-        up_project_and_store(LAST, FIRST, psum_c.tile([P, LATENT], F32, name="latent_ps"), nc.scalar.copy)
+        kv_ps = psum_one.tile([P, TILES * KV_OUT], F32, name="kv_ps")
+        up_project_and_store(LAST - 1, BOTH, kv_ps, nc.scalar.copy, nc.scalar)
+        up_project_and_store(LAST, FIRST, psum_c.tile([P, LATENT], F32, name="latent_ps"), nc.scalar.copy, nc.scalar)
         up_project_and_store(LAST, SECOND, psum_c.tile([P, LATENT], F32, name="latent_ps"), nc.vector.tensor_copy)

@@ -52,8 +52,8 @@ def tile_multiheadlatentattention_pb_t_kernel(tc, x, w_dkv, kv_a_norm, w_ukv, ou
         x_pool = ctx.enter_context(tc.tile_pool(name="x_pool", bufs=ROUNDS))
         work = ctx.enter_context(tc.tile_pool(name="work", bufs=4))
         psum_x = ctx.enter_context(tc.psum_pool(name="psum_x", bufs=2))
-        psum_c = ctx.enter_context(tc.psum_pool(name="psum_c", bufs=3))
-        psum_one = ctx.enter_context(tc.psum_pool(name="psum_one", bufs=1))
+        psum_key = ctx.enter_context(tc.psum_pool(name="psum_key", bufs=1))
+        psum_mix = ctx.enter_context(tc.psum_pool(name="psum_mix", bufs=5))
         ctx.enter_context(tc.manual_schedule())
 
         n_pos = SEQ // P
@@ -176,16 +176,18 @@ def tile_multiheadlatentattention_pb_t_kernel(tc, x, w_dkv, kv_a_norm, w_ukv, ou
 
         gain = keep.tile([P, LATENT], BF16)
 
-        gain_ps = psum_one.tile([P, 2 * TILES, P], F32, name="ht_ps")
+        def take_bank():
+            return psum_mix.tile([P, LATENT], F32, name="bank")
+
+        gain_ps = take_bank()
 
         def spread_gain():
-            gain_cols = gain_ps[:].rearrange("p n r -> p (n r)")
-            nc.tensor.matmul(gain_cols, lhsT=ones[:], rhs=gain_row[:], start=True, stop=True)
+            nc.tensor.matmul(gain_ps[:], lhsT=ones[:], rhs=gain_row[:], start=True, stop=True)
 
         def copy_gain():
             nc.vector.tensor_copy(
                 out=gain[:].rearrange("p (u q e) -> p u q e", u=2, e=2),
-                in_=gain_ps[:].rearrange("p n r -> p (n r)").rearrange("p (q u e) -> p u q e", u=2, e=2),
+                in_=gain_ps[:].rearrange("p (q u e) -> p u q e", u=2, e=2),
             )
 
         wu_grouped = keep.tile([P, KV_OUT, PACK], BF16, align_bytes=64)
@@ -204,7 +206,7 @@ def tile_multiheadlatentattention_pb_t_kernel(tc, x, w_dkv, kv_a_norm, w_ukv, ou
 
         x_grouped, x_codes, x_scales = {}, {}, {}
         latent_ps, key_ps, sum_sq, inv_rms = {}, {}, {}, {}
-        h_sb, h_grouped, h_codes, h_scales = {}, {}, {}, {}
+        h_sb, h_grouped, h_codes, h_scales, kv_ps = {}, {}, {}, {}, {}
 
         def transpose_x(i):
             words = x_sb[i][:].bitcast(F32)
@@ -244,11 +246,11 @@ def tile_multiheadlatentattention_pb_t_kernel(tc, x, w_dkv, kv_a_norm, w_ukv, ou
                     stop=(g == X_PASSES - 1),
                 )
 
-        def project_latent(i, n):
+        def project_latent(i, n, bank):
             if n == 0:
                 sum_sq[i] = work.tile([P, TILES], F32, name="sum_sq")
                 inv_rms[i] = work.tile([P, TILES], F32, name="inv_rms")
-            latent_ps[i, n] = psum_c.tile([P, LATENT], F32, name="latent_ps")
+            latent_ps[i, n] = bank
             multiply_down(latent_ps[i, n][:], i, n, LATENT_COLS)
             squares = work.tile([P, LATENT], BF16, name="squares")
             nc.scalar.activation(
@@ -256,7 +258,7 @@ def tile_multiheadlatentattention_pb_t_kernel(tc, x, w_dkv, kv_a_norm, w_ukv, ou
             )
 
         def project_key(i):
-            key_ps[i] = psum_one.tile([P, TILES, ROPE], F32, name="key_ps")
+            key_ps[i] = psum_key.tile([P, TILES, ROPE], F32, name="key_ps")
             for n in range(TILES):
                 multiply_down(key_ps[i][:, n, :], i, n, KEY_COLS)
 
@@ -304,16 +306,18 @@ def tile_multiheadlatentattention_pb_t_kernel(tc, x, w_dkv, kv_a_norm, w_ukv, ou
                 op1=ALU.mult,
             )
 
-        def transpose_h(i, tiles, ht_ps, copy):
+        def transpose_h(i, tiles, bank, copy):
             if tiles.start == 0:
                 h_grouped[i] = work.tile([P, TILES, 2 * P], F32, name="h_grouped", align_bytes=64)
-            for j, n in enumerate(range(tiles.start, tiles.stop)):
-                words = h_sb[i][:, n, :].bitcast(F32)
+            count = tiles.stop - tiles.start
+            ht_ps = bank[:, 0 : count * 2 * P].rearrange("p (n u r) -> p n u r", u=2, r=P)
+            for j in range(count):
+                words = h_sb[i][:, tiles.start + j, :].bitcast(F32)
                 for u in range(2):
-                    nc.tensor.transpose(ht_ps[:, 2 * j + u, :], words[:, u * P : (u + 1) * P], identity[:])
+                    nc.tensor.transpose(ht_ps[:, j, u, :], words[:, u * P : (u + 1) * P], identity[:])
             copy(
                 out=h_grouped[i][:, tiles, :].rearrange("p n (r u) -> p n r u", u=2),
-                in_=ht_ps[:, 0 : 2 * (tiles.stop - tiles.start), :].rearrange("p (n u) r -> p n r u", u=2),
+                in_=ht_ps.rearrange("p n u r -> p n r u"),
             )
 
         def quantise_h(i, tiles):
@@ -326,11 +330,11 @@ def tile_multiheadlatentattention_pb_t_kernel(tc, x, w_dkv, kv_a_norm, w_ukv, ou
                 in_=h_grouped[i][:, tiles, :].rearrange("p n w -> p (n w)").bitcast(BF16),
             )
 
-        def up_project_and_store(i, tiles, kv_ps, copy, queue=nc.sync):
-            count = tiles.stop - tiles.start
+        def up_project(i, tiles, out):
+            kv_ps[i, tiles.start] = out
             for j, n in enumerate(range(tiles.start, tiles.stop)):
                 nc.tensor.matmul_mx(
-                    out=kv_ps[:, j * KV_OUT : (j + 1) * KV_OUT],
+                    out=out[:, j * KV_OUT : (j + 1) * KV_OUT],
                     lhsT=h_codes[i][:, n, :].bitcast(FP8X4),
                     lhsT_scale=h_scales[i][:, n, :],
                     rhs=wu_codes[:].bitcast(FP8X4),
@@ -338,10 +342,13 @@ def tile_multiheadlatentattention_pb_t_kernel(tc, x, w_dkv, kv_a_norm, w_ukv, ou
                     start=True,
                     stop=True,
                 )
+
+        def store_kv(i, tiles, copy, queue=nc.sync):
+            count = tiles.stop - tiles.start
             kv_sb = work.tile([P, 2, count, HEADS, NOPE], F32, name="kv_sb")
             copy(
                 out=kv_sb[:].rearrange("p a n h f -> p (n h) a f"),
-                in_=kv_ps[:, 0 : count * KV_OUT].rearrange("p (m a f) -> p m a f", a=2, f=NOPE),
+                in_=kv_ps[i, tiles.start][:, 0 : count * KV_OUT].rearrange("p (m a f) -> p m a f", a=2, f=NOPE),
             )
             rows = slice(i * ROUND, (i + 1) * ROUND)
             kf = kf_rows[rows].rearrange("(p n) h f -> p n h f", n=TILES)
@@ -371,17 +378,16 @@ def tile_multiheadlatentattention_pb_t_kernel(tc, x, w_dkv, kv_a_norm, w_ukv, ou
             r_x, r_c, r_h, r_t, r_kv = step, step - 1, step - 2, step - 3, step - 4
             if 0 <= r_h < LAST:
                 rotate_and_store(r_h)
+            if 0 <= r_h:
                 for n in range(TILES):
                     normalise(r_h, n)
-            elif r_h == LAST:
-                for n in range(TILES):
-                    normalise(LAST, n)
+            if r_h == LAST:
                 rotate_and_store(LAST)
-            if 0 <= r_t < LAST:
-                transpose_h(r_t, BOTH, psum_one.tile([P, 2 * TILES, P], F32, name="ht_ps"), nc.scalar.copy)
+            if 0 <= r_t:
+                transpose_h(r_t, BOTH, take_bank(), nc.scalar.copy)
             if r_x < ROUNDS:
                 transpose_x(r_x)
-            if 0 <= r_t < LAST:
+            if 0 <= r_t:
                 quantise_h(r_t, BOTH)
             if r_x < ROUNDS:
                 quantise_x(r_x)
@@ -389,28 +395,34 @@ def tile_multiheadlatentattention_pb_t_kernel(tc, x, w_dkv, kv_a_norm, w_ukv, ou
                 group_up_weights()
             if step == 3:
                 quantise_up_weights()
-            if 0 <= r_c < LAST:
-                for n in range(TILES):
-                    project_latent(r_c, n)
-                invert_rms(r_c, BOTH)
+            if r_c < LAST:
+                first_bank = take_bank()
+                kv_bank = take_bank() if 0 <= r_kv else None
+                second_bank = take_bank()
+                project_latent(r_c, 0, first_bank)
+                project_latent(r_c, 1, second_bank)
+                invert_rms(r_c, FIRST)
                 project_key(r_c)
-            elif r_c == LAST:
-                project_latent(LAST, 0)
-                invert_rms(LAST, FIRST)
-                up_project_and_store(
-                    r_kv, BOTH, psum_one.tile([P, TILES * KV_OUT], F32, name="kv_ps"), nc.vector.tensor_copy
-                )
-                project_latent(LAST, 1)
-                invert_rms(LAST, SECOND)
-                project_key(LAST)
-            if 0 <= r_kv and step != ROUNDS:
-                up_project_and_store(r_kv, BOTH, psum_one.tile([P, TILES * KV_OUT], F32, name="kv_ps"), nc.scalar.copy)
+                if 0 <= r_kv:
+                    up_project(r_kv, BOTH, kv_bank)
+                    store_kv(r_kv, BOTH, nc.scalar.copy)
+                invert_rms(r_c, SECOND)
+            else:
+                up_project(r_kv, BOTH, take_bank())
+                store_kv(r_kv, BOTH, nc.scalar.copy)
+                if r_c == LAST:
+                    for n, tile in enumerate((FIRST, SECOND)):
+                        project_latent(LAST, n, take_bank())
+                        invert_rms(LAST, tile)
+                    project_key(LAST)
 
-        transpose_h(LAST, FIRST, psum_one.tile([P, 2 * TILES, P], F32, name="ht_ps"), nc.scalar.copy)
+        transpose_h(LAST, FIRST, take_bank(), nc.scalar.copy)
         quantise_h(LAST, FIRST)
-        transpose_h(LAST, SECOND, psum_x.tile([P, 2 * X_PASSES, P], F32, name="xt_ps"), nc.vector.tensor_copy)
+        transpose_h(LAST, SECOND, take_bank(), nc.vector.tensor_copy)
         quantise_h(LAST, SECOND)
-        kv_ps = psum_one.tile([P, TILES * KV_OUT], F32, name="kv_ps")
-        up_project_and_store(LAST - 1, BOTH, kv_ps, nc.scalar.copy, nc.scalar)
-        up_project_and_store(LAST, FIRST, psum_c.tile([P, LATENT], F32, name="latent_ps"), nc.scalar.copy, nc.scalar)
-        up_project_and_store(LAST, SECOND, psum_c.tile([P, LATENT], F32, name="latent_ps"), nc.vector.tensor_copy)
+        up_project(LAST - 1, BOTH, take_bank())
+        store_kv(LAST - 1, BOTH, nc.scalar.copy, nc.scalar)
+        up_project(LAST, FIRST, take_bank())
+        store_kv(LAST, FIRST, nc.scalar.copy, nc.scalar)
+        up_project(LAST, SECOND, take_bank())
+        store_kv(LAST, SECOND, nc.vector.tensor_copy)

@@ -218,7 +218,7 @@ def tile_multiheadlatentattention_pb_t_kernel(tc, x, w_dkv, kv_a_norm, w_ukv, ou
                     g, u = divmod(a, 2)
                     start = n * n_words + g * 2 * P
                     nc.tensor.transpose(xt_ps[:, a, :], words[:, start + u : start + 2 * P : 2], identity[:])
-                copy = nc.scalar.copy if (n == 0 and i != 1) or i % 4 == 0 else nc.vector.tensor_copy
+                copy = nc.scalar.copy if (n == 0 and i != 1) or i % 4 == 0 or i in (2, 3) else nc.vector.tensor_copy
                 copy(
                     out=x_grouped[i][:, n * n_words : (n + 1) * n_words].rearrange(
                         "p (g r u) -> p g r u", g=X_PASSES, u=2
@@ -379,19 +379,18 @@ def tile_multiheadlatentattention_pb_t_kernel(tc, x, w_dkv, kv_a_norm, w_ukv, ou
             if 0 <= r_h < LAST:
                 rotate_and_store(r_h)
             if 0 <= r_h:
-                for n in range(TILES):
-                    normalise(r_h, n)
-            if r_h == LAST:
-                rotate_and_store(LAST)
+                normalise(r_h, 0)
+            if r_x < ROUNDS:
+                transpose_x(r_x)
+            if 0 <= r_h:
+                normalise(r_h, 1)
             if 0 <= r_t:
                 transpose_h(r_t, BOTH, take_bank(), nc.scalar.copy)
             if r_x < ROUNDS:
-                transpose_x(r_x)
+                quantise_x(r_x)
             if 0 <= r_t:
                 quantise_h(r_t, BOTH)
-            if r_x < ROUNDS:
-                quantise_x(r_x)
-            if step == 2:
+            if step == 1:
                 group_up_weights()
             if step == 3:
                 quantise_up_weights()
@@ -409,12 +408,15 @@ def tile_multiheadlatentattention_pb_t_kernel(tc, x, w_dkv, kv_a_norm, w_ukv, ou
                 invert_rms(r_c, SECOND)
             else:
                 up_project(r_kv, BOTH, take_bank())
+                if r_c == LAST:
+                    project_latent(LAST, 0, take_bank())
+                    invert_rms(LAST, FIRST)
+                    project_key(LAST)
                 store_kv(r_kv, BOTH, nc.scalar.copy)
                 if r_c == LAST:
-                    for n, tile in enumerate((FIRST, SECOND)):
-                        project_latent(LAST, n, take_bank())
-                        invert_rms(LAST, tile)
-                    project_key(LAST)
+                    project_latent(LAST, 1, take_bank())
+                    invert_rms(LAST, SECOND)
+                    rotate_and_store(LAST)
 
         transpose_h(LAST, FIRST, take_bank(), nc.scalar.copy)
         quantise_h(LAST, FIRST)

@@ -85,9 +85,9 @@ def tile_multiheadlatentattention_pb_t_kernel(tc, x, w_dkv, kv_a_norm, w_ukv, ou
                 in_=w_dkv[g * K_PASS : (g + 1) * K_PASS, :].rearrange("(p t) c -> p (t c)", t=PACK),
             )
 
+        load_down_weights(0)
         load_x(0)
-        for g in range(X_PASSES):
-            load_down_weights(g)
+        load_down_weights(1)
         gain_row = keep.tile([P, LATENT], BF16)
         nc.gpsimd.memset(gain_row[:].bitcast(I32), 0)
         ones = keep.tile([P, P], BF16)
@@ -136,9 +136,9 @@ def tile_multiheadlatentattention_pb_t_kernel(tc, x, w_dkv, kv_a_norm, w_ukv, ou
         eps = keep.tile([P, 1], F32)
         nc.gpsimd.tensor_scalar_mul(out=eps[:], in0=one[:], scalar1=EPS)
         abs_turns = keep.tile(table_shape, F32)
+        nc.scalar.activation(out=abs_turns[:], in_=turns[:], func=ACT.Abs)
 
         def make_cosines():
-            nc.scalar.activation(out=abs_turns[:], in_=turns[:], func=ACT.Abs)
             nc.scalar.activation(
                 out=trig[:, :, 0, :], in_=abs_turns[:], func=ACT.Sin, bias=quarter_turn[:], scale=-2.0 * math.pi
             )
@@ -218,7 +218,7 @@ def tile_multiheadlatentattention_pb_t_kernel(tc, x, w_dkv, kv_a_norm, w_ukv, ou
                     g, u = divmod(a, 2)
                     start = n * n_words + g * 2 * P
                     nc.tensor.transpose(xt_ps[:, a, :], words[:, start + u : start + 2 * P : 2], identity[:])
-                copy = nc.scalar.copy if (n == 0 and i != 1) or i % 4 == 0 or i in (2, 3) else nc.vector.tensor_copy
+                copy = nc.scalar.copy if (n == 0 and i != 2) or i % 4 == 0 or i in (1, 3) else nc.vector.tensor_copy
                 copy(
                     out=x_grouped[i][:, n * n_words : (n + 1) * n_words].rearrange(
                         "p (g r u) -> p g r u", g=X_PASSES, u=2
@@ -363,10 +363,9 @@ def tile_multiheadlatentattention_pb_t_kernel(tc, x, w_dkv, kv_a_norm, w_ukv, ou
         spread_gain()
         quantise_weights(0, LATENT_COLS)
         make_cosines()
-        load_root_table()
         group_latent_weights(1)
-        quantise_x(0)
         quantise_weights(1, LATENT_COLS)
+        quantise_x(0)
         for g in range(X_PASSES):
             group_key_weights(g)
         for g in range(X_PASSES):
@@ -378,9 +377,11 @@ def tile_multiheadlatentattention_pb_t_kernel(tc, x, w_dkv, kv_a_norm, w_ukv, ou
             r_x, r_c, r_h, r_t, r_kv = step, step - 1, step - 2, step - 3, step - 4
             if 0 <= r_h < LAST:
                 rotate_and_store(r_h)
+            if step == 2:
+                transpose_x(r_x)
             if 0 <= r_h:
                 normalise(r_h, 0)
-            if r_x < ROUNDS:
+            if r_x < ROUNDS and step != 2:
                 transpose_x(r_x)
             if 0 <= r_h:
                 normalise(r_h, 1)
@@ -391,7 +392,7 @@ def tile_multiheadlatentattention_pb_t_kernel(tc, x, w_dkv, kv_a_norm, w_ukv, ou
             if 0 <= r_t:
                 quantise_h(r_t, BOTH)
             if step == 1:
-                group_up_weights()
+                load_root_table()
             if step == 3:
                 quantise_up_weights()
             if r_c < LAST:
@@ -406,6 +407,8 @@ def tile_multiheadlatentattention_pb_t_kernel(tc, x, w_dkv, kv_a_norm, w_ukv, ou
                     up_project(r_kv, BOTH, kv_bank)
                     store_kv(r_kv, BOTH, nc.scalar.copy)
                 invert_rms(r_c, SECOND)
+                if step == 2:
+                    group_up_weights()
             else:
                 up_project(r_kv, BOTH, take_bank())
                 if r_c == LAST:

import math
from contextlib import ExitStack

import concourse.mybir as mybir
from concourse.masks import make_identity

F32 = mybir.dt.float32
BF16 = mybir.dt.bfloat16
I32 = mybir.dt.int32
U32 = mybir.dt.uint32
U8 = mybir.dt.uint8
FP8X4 = mybir.dt.float8_e4m3fn_x4
ALU = mybir.AluOpType
ACT = mybir.ActivationFunctionType

P = 128
PACK = 4
K_PASS = P * PACK

TOKENS = 2 * 2048
SEQ = 2048
D_MODEL = 1024
LATENT = 512
ROPE = 128
HALF = ROPE // 2
HEADS = 2
NOPE = 64
V_DIM = 64
KV_OUT = HEADS * (NOPE + V_DIM)
EPS = 1e-6
THETA = 10000.0

X_PASSES = D_MODEL // K_PASS
TILES = 2
ROUND = TILES * P
ROUNDS = TOKENS // ROUND
SEQ_ROUNDS = SEQ // ROUND

ROUND_MAGIC = 12582912.0

FLOPS = 2 * TOKENS * D_MODEL * (LATENT + ROPE) + 2 * TOKENS * LATENT * KV_OUT


def tile_multiheadlatentattention_pb_t_kernel(tc, x, w_dkv, kv_a_norm, w_ukv, out_0, out_1):
    nc = tc.nc
    x_rows = x.flatten_outer_dims()
    kf_rows = out_0.rearrange("b s h f -> (b s) h f")
    v_rows = out_1.rearrange("b s h f -> (b s) (h f)")

    with ExitStack() as ctx:
        keep = ctx.enter_context(tc.tile_pool(name="keep", bufs=1))
        x_pool = ctx.enter_context(tc.tile_pool(name="x_pool", bufs=ROUNDS))
        work = ctx.enter_context(tc.tile_pool(name="work", bufs=4))
        psum_x = ctx.enter_context(tc.psum_pool(name="psum_x", bufs=2))
        psum_key = ctx.enter_context(tc.psum_pool(name="psum_key", bufs=1))
        psum_mix = ctx.enter_context(tc.psum_pool(name="psum_mix", bufs=5))
        ctx.enter_context(tc.manual_schedule())

        n_pos = SEQ // P
        pos = keep.tile([P, n_pos], F32)
        nc.gpsimd.iota(
            pos[:],
            pattern=[[ROUND, SEQ_ROUNDS], [1, TILES]],
            base=0,
            channel_multiplier=TILES,
            allow_small_or_imprecise_dtypes=True,
        )
        identity = keep.tile([P, P], F32)
        make_identity(nc, identity[:])

        x_sb = {}

        def load_x(i):
            x_sb[i] = x_pool.tile([P, TILES * D_MODEL], BF16, name="x_sb")
            nc.sync.dma_start(
                out=x_sb[i][:],
                in_=x_rows[i * ROUND : (i + 1) * ROUND, :].rearrange("(p n) d -> p (n d)", n=TILES),
            )

        wd_raw = keep.tile([P, X_PASSES, PACK, LATENT + ROPE], BF16)

        def load_down_weights(g):
            nc.sync.dma_start(
                out=wd_raw[:, g].rearrange("p t c -> p (t c)"),
                in_=w_dkv[g * K_PASS : (g + 1) * K_PASS, :].rearrange("(p t) c -> p (t c)", t=PACK),
            )

        load_down_weights(0)
        load_x(0)
        load_down_weights(1)
        gain_row = keep.tile([P, LATENT], BF16)
        nc.gpsimd.memset(gain_row[:].bitcast(I32), 0)
        ones = keep.tile([P, P], BF16)
        nc.gpsimd.memset(ones[:], 1.0)
        nc.sync.dma_start(out=gain_row[0:1, :], in_=kv_a_norm.unsqueeze(0))
        load_x(1)
        wu_raw = keep.tile([P, PACK, KV_OUT], BF16)
        nc.sync.dma_start(
            out=wu_raw[:].rearrange("p t n -> p (t n)"),
            in_=w_ukv.rearrange("(p t) n -> p (t n)", t=PACK),
        )
        for i in range(2, ROUNDS):
            load_x(i)

        table_shape = [P, n_pos, HALF]
        turns = keep.tile(table_shape, F32)
        nc.vector.tensor_scalar_mul(out=turns[:, :, 0:1], in0=pos[:].unsqueeze(2), scalar1=1.0 / (2.0 * math.pi))
        filled = 1
        while filled < HALF:
            for part in range(1, 4):
                nc.vector.tensor_scalar_mul(
                    out=turns[:, :, part * filled : (part + 1) * filled],
                    in0=turns[:, :, 0:filled],
                    scalar1=THETA ** (-part * filled / HALF),
                )
            filled *= 4
        fast = sum(1 for i in range(HALF) if SEQ * THETA ** (-i / HALF) > math.pi)
        whole = keep.tile([P, n_pos, fast], F32)
        nc.vector.tensor_scalar(
            out=whole[:],
            in0=turns[:, :, 0:fast],
            scalar1=ROUND_MAGIC,
            scalar2=ROUND_MAGIC,
            op0=ALU.add,
            op1=ALU.subtract,
        )
        nc.vector.tensor_tensor(
            out=turns[:, :, 0:fast], in0=turns[:, :, 0:fast], in1=whole[:], op=ALU.subtract
        )
        trig = keep.tile([P, n_pos, 2, HALF], F32)
        nc.scalar.activation(out=trig[:, :, 1, :], in_=turns[:], func=ACT.Sin, scale=2.0 * math.pi)
        one = keep.tile([P, 1], F32)
        nc.gpsimd.memset(one[:], 1.0)
        quarter_turn = keep.tile([P, 1], F32)
        nc.gpsimd.tensor_scalar_mul(out=quarter_turn[:], in0=one[:], scalar1=math.pi / 2.0)
        eps = keep.tile([P, 1], F32)
        nc.gpsimd.tensor_scalar_mul(out=eps[:], in0=one[:], scalar1=EPS)
        abs_turns = keep.tile(table_shape, F32)
        nc.scalar.activation(out=abs_turns[:], in_=turns[:], func=ACT.Abs)

        def make_cosines():
            nc.scalar.activation(
                out=trig[:, :, 0, :], in_=abs_turns[:], func=ACT.Sin, bias=quarter_turn[:], scale=-2.0 * math.pi
            )

        inv_scratch = keep.tile([P, 1], F32)

        def load_root_table():
            nc.scalar.activation(out=inv_scratch[:], in_=one[:], func=ACT.Abs_reciprocal_sqrt)

        wd_grouped = keep.tile([P, X_PASSES, LATENT + ROPE, PACK], BF16, align_bytes=64)
        wd_codes = keep.tile([P, X_PASSES, LATENT + ROPE], U32, align_bytes=64)
        wd_scales = keep.tile([P, X_PASSES, LATENT + ROPE], U8, align_bytes=64)

        def group_latent_weights(g):
            for u in range(2):
                nc.vector.tensor_copy(
                    out=wd_grouped[:, g, 2 * P * u : 2 * P * (u + 1)].rearrange("p (q e) t -> p q t e", e=2),
                    in_=wd_raw[:, g, :, 0:LATENT].rearrange("p t (q u e) -> p q u t e", u=2, e=2)[:, :, u],
                )

        def group_key_weights(g):
            nc.vector.tensor_copy(
                out=wd_grouped[:, g, LATENT : LATENT + ROPE].rearrange("p (c i) t -> p c t i", i=4),
                in_=wd_raw[:, g, :, LATENT : LATENT + ROPE].rearrange("p t (c i) -> p c t i", i=4),
            )

        def quantise_weights(g, cols):
            nc.vector.quantize_mx(
                out=wd_codes[:, g, cols].bitcast(FP8X4),
                scales=wd_scales[:, g, cols],
                in_=wd_grouped[:, g, cols, :].rearrange("p c t -> p (c t)"),
            )

        LATENT_COLS, KEY_COLS = slice(0, LATENT), slice(LATENT, LATENT + ROPE)

        gain = keep.tile([P, LATENT], BF16)

        def take_bank():
            return psum_mix.tile([P, LATENT], F32, name="bank")

        gain_ps = take_bank()

        def spread_gain():
            nc.tensor.matmul(gain_ps[:], lhsT=ones[:], rhs=gain_row[:], start=True, stop=True)

        def copy_gain():
            nc.vector.tensor_copy(
                out=gain[:].rearrange("p (u q e) -> p u q e", u=2, e=2),
                in_=gain_ps[:].rearrange("p (q u e) -> p u q e", u=2, e=2),
            )

        wu_grouped = keep.tile([P, KV_OUT, PACK], BF16, align_bytes=64)
        wu_codes = keep.tile([P, KV_OUT], U32, align_bytes=64)
        wu_scales = keep.tile([P, KV_OUT], U8, align_bytes=64)

        def group_up_weights():
            nc.scalar.copy(out=wu_grouped[:], in_=wu_raw[:].rearrange("p t n -> p n t"))

        def quantise_up_weights():
            nc.vector.quantize_mx(
                out=wu_codes[:].bitcast(FP8X4),
                scales=wu_scales[:],
                in_=wu_grouped[:].rearrange("p n t -> p (n t)"),
            )

        x_grouped, x_codes, x_scales = {}, {}, {}
        latent_ps, key_ps, sum_sq, inv_rms = {}, {}, {}, {}
        h_sb, h_grouped, h_codes, h_scales, kv_ps = {}, {}, {}, {}, {}

        def transpose_x(i):
            words = x_sb[i][:].bitcast(F32)
            n_words = D_MODEL // 2
            x_grouped[i] = work.tile([P, TILES * n_words], F32, name="x_grouped", align_bytes=64)
            for n in range(TILES):
                xt_ps = psum_x.tile([P, 2 * X_PASSES, P], F32, name="xt_ps")
                for a in range(2 * X_PASSES):
                    g, u = divmod(a, 2)
                    start = n * n_words + g * 2 * P
                    nc.tensor.transpose(xt_ps[:, a, :], words[:, start + u : start + 2 * P : 2], identity[:])
                copy = nc.scalar.copy if (n == 0 and i != 2) or i % 4 == 0 or i in (1, 3) else nc.vector.tensor_copy
                copy(
                    out=x_grouped[i][:, n * n_words : (n + 1) * n_words].rearrange(
                        "p (g r u) -> p g r u", g=X_PASSES, u=2
                    ),
                    in_=xt_ps[:].rearrange("p (g u) r -> p g r u", u=2),
                )

        def quantise_x(i):
            x_codes[i] = work.tile([P, TILES * X_PASSES * P], U32, name="x_codes", align_bytes=64)
            x_scales[i] = work.tile([P, TILES * X_PASSES * P], U8, name="x_scales", align_bytes=64)
            nc.vector.quantize_mx(
                out=x_codes[i][:].bitcast(FP8X4), scales=x_scales[i][:], in_=x_grouped[i][:].bitcast(BF16)
            )

        def multiply_down(out, i, n, cols):
            for g in range(X_PASSES):
                tokens = slice((n * X_PASSES + g) * P, (n * X_PASSES + g + 1) * P)
                nc.tensor.matmul_mx(
                    out=out,
                    lhsT=x_codes[i][:, tokens].bitcast(FP8X4),
                    lhsT_scale=x_scales[i][:, tokens],
                    rhs=wd_codes[:, g, cols].bitcast(FP8X4),
                    rhs_scale=wd_scales[:, g, cols],
                    start=(g == 0),
                    stop=(g == X_PASSES - 1),
                )

        def project_latent(i, n, bank):
            if n == 0:
                sum_sq[i] = work.tile([P, TILES], F32, name="sum_sq")
                inv_rms[i] = work.tile([P, TILES], F32, name="inv_rms")
            latent_ps[i, n] = bank
            multiply_down(latent_ps[i, n][:], i, n, LATENT_COLS)
            squares = work.tile([P, LATENT], BF16, name="squares")
            nc.scalar.activation(
                out=squares[:], in_=latent_ps[i, n][:], func=ACT.Square, accum_out=sum_sq[i][:, n : n + 1]
            )

        def project_key(i):
            key_ps[i] = psum_key.tile([P, TILES, ROPE], F32, name="key_ps")
            for n in range(TILES):
                multiply_down(key_ps[i][:, n, :], i, n, KEY_COLS)

        def invert_rms(i, tiles):
            nc.scalar.activation(
                out=inv_rms[i][:, tiles],
                in_=sum_sq[i][:, tiles],
                func=ACT.Abs_reciprocal_sqrt,
                bias=eps[:],
                scale=1.0 / LATENT,
            )

        def rotate_and_store(i):
            first = (i % SEQ_ROUNDS) * TILES
            shape = [P, TILES, 2, 2, HALF]
            products = work.tile(shape, F32, name="products")
            nc.vector.tensor_tensor(
                out=products[:],
                in0=key_ps[i][:].rearrange("p n (a f) -> p n a f", a=2).unsqueeze(2).to_broadcast(shape),
                in1=trig[:, first : first + TILES].unsqueeze(3).to_broadcast(shape),
                op=ALU.mult,
            )
            rotated = work.tile([P, TILES, 2, HALF], F32, name="rotated")
            nc.gpsimd.tensor_tensor(
                out=rotated[:, :, 0, :], in0=products[:, :, 0, 0, :], in1=products[:, :, 1, 1, :], op=ALU.subtract
            )
            nc.gpsimd.tensor_tensor(
                out=rotated[:, :, 1, :], in0=products[:, :, 0, 1, :], in1=products[:, :, 1, 0, :], op=ALU.add
            )
            kf = kf_rows[i * ROUND : (i + 1) * ROUND].rearrange("(p n) h f -> p n h f", n=TILES)
            for head in range(HEADS):
                nc.sync.dma_start(
                    out=kf[:, :, head, NOPE : NOPE + ROPE], in_=rotated[:].rearrange("p n a f -> p n (a f)")
                )

        def normalise(i, n):
            if n == 0:
                h_sb[i] = work.tile([P, TILES, LATENT], BF16, name="h_sb")
            nc.vector.scalar_tensor_tensor(
                out=h_sb[i][:, n, :],
                in0=latent_ps[i, n][:],
                scalar=inv_rms[i][:, n : n + 1],
                in1=gain[:],
                op0=ALU.mult,
                op1=ALU.mult,
            )

        def transpose_h(i, tiles, bank, copy):
            if tiles.start == 0:
                h_grouped[i] = work.tile([P, TILES, 2 * P], F32, name="h_grouped", align_bytes=64)
            count = tiles.stop - tiles.start
            ht_ps = bank[:, 0 : count * 2 * P].rearrange("p (n u r) -> p n u r", u=2, r=P)
            for j in range(count):
                words = h_sb[i][:, tiles.start + j, :].bitcast(F32)
                for u in range(2):
                    nc.tensor.transpose(ht_ps[:, j, u, :], words[:, u * P : (u + 1) * P], identity[:])
            copy(
                out=h_grouped[i][:, tiles, :].rearrange("p n (r u) -> p n r u", u=2),
                in_=ht_ps.rearrange("p n u r -> p n r u"),
            )

        def quantise_h(i, tiles):
            if tiles.start == 0:
                h_codes[i] = work.tile([P, TILES, P], U32, name="h_codes", align_bytes=64)
                h_scales[i] = work.tile([P, TILES, P], U8, name="h_scales", align_bytes=64)
            nc.vector.quantize_mx(
                out=h_codes[i][:, tiles, :].rearrange("p n r -> p (n r)").bitcast(FP8X4),
                scales=h_scales[i][:, tiles, :].rearrange("p n r -> p (n r)"),
                in_=h_grouped[i][:, tiles, :].rearrange("p n w -> p (n w)").bitcast(BF16),
            )

        def up_project(i, tiles, out):
            kv_ps[i, tiles.start] = out
            for j, n in enumerate(range(tiles.start, tiles.stop)):
                nc.tensor.matmul_mx(
                    out=out[:, j * KV_OUT : (j + 1) * KV_OUT],
                    lhsT=h_codes[i][:, n, :].bitcast(FP8X4),
                    lhsT_scale=h_scales[i][:, n, :],
                    rhs=wu_codes[:].bitcast(FP8X4),
                    rhs_scale=wu_scales[:],
                    start=True,
                    stop=True,
                )

        def store_kv(i, tiles, copy, queue=nc.sync):
            count = tiles.stop - tiles.start
            kv_sb = work.tile([P, 2, count, HEADS, NOPE], F32, name="kv_sb")
            copy(
                out=kv_sb[:].rearrange("p a n h f -> p (n h) a f"),
                in_=kv_ps[i, tiles.start][:, 0 : count * KV_OUT].rearrange("p (m a f) -> p m a f", a=2, f=NOPE),
            )
            rows = slice(i * ROUND, (i + 1) * ROUND)
            kf = kf_rows[rows].rearrange("(p n) h f -> p n h f", n=TILES)
            queue.dma_start(out=kf[:, tiles, :, 0:NOPE], in_=kv_sb[:, 0])
            v = v_rows[rows].rearrange("(p n) f -> p n f", n=TILES)
            queue.dma_start(out=v[:, tiles, :], in_=kv_sb[:, 1].rearrange("p n h f -> p n (h f)"))

        BOTH, FIRST, SECOND = slice(0, 2), slice(0, 1), slice(1, 2)

        group_latent_weights(0)
        transpose_x(0)
        spread_gain()
        quantise_weights(0, LATENT_COLS)
        make_cosines()
        group_latent_weights(1)
        quantise_weights(1, LATENT_COLS)
        quantise_x(0)
        for g in range(X_PASSES):
            group_key_weights(g)
        for g in range(X_PASSES):
            quantise_weights(g, KEY_COLS)
        copy_gain()

        LAST = ROUNDS - 1
        for step in range(1, ROUNDS + 2):
            r_x, r_c, r_h, r_t, r_kv = step, step - 1, step - 2, step - 3, step - 4
            if 0 <= r_h < LAST:
                rotate_and_store(r_h)
            if step == 2:
                transpose_x(r_x)
            if 0 <= r_h:
                normalise(r_h, 0)
            if r_x < ROUNDS and step != 2:
                transpose_x(r_x)
            if 0 <= r_h:
                normalise(r_h, 1)
            if 0 <= r_t:
                transpose_h(r_t, BOTH, take_bank(), nc.scalar.copy)
            if r_x < ROUNDS:
                quantise_x(r_x)
            if 0 <= r_t:
                quantise_h(r_t, BOTH)
            if step == 1:
                load_root_table()
            if step == 3:
                quantise_up_weights()
            if r_c < LAST:
                first_bank = take_bank()
                kv_bank = take_bank() if 0 <= r_kv else None
                second_bank = take_bank()
                project_latent(r_c, 0, first_bank)
                project_latent(r_c, 1, second_bank)
                invert_rms(r_c, FIRST)
                project_key(r_c)
                if 0 <= r_kv:
                    up_project(r_kv, BOTH, kv_bank)
                    store_kv(r_kv, BOTH, nc.scalar.copy)
                invert_rms(r_c, SECOND)
                if step == 2:
                    group_up_weights()
            else:
                up_project(r_kv, BOTH, take_bank())
                if r_c == LAST:
                    project_latent(LAST, 0, take_bank())
                    invert_rms(LAST, FIRST)
                    project_key(LAST)
                store_kv(r_kv, BOTH, nc.scalar.copy)
                if r_c == LAST:
                    project_latent(LAST, 1, take_bank())
                    invert_rms(LAST, SECOND)
                    rotate_and_store(LAST)

        transpose_h(LAST, FIRST, take_bank(), nc.scalar.copy)
        quantise_h(LAST, FIRST)
        transpose_h(LAST, SECOND, take_bank(), nc.vector.tensor_copy)
        quantise_h(LAST, SECOND)
        up_project(LAST - 1, BOTH, take_bank())
        store_kv(LAST - 1, BOTH, nc.scalar.copy, nc.scalar)
        up_project(LAST, FIRST, take_bank())
        store_kv(LAST, FIRST, nc.scalar.copy, nc.scalar)
        up_project(LAST, SECOND, take_bank())
        store_kv(LAST, SECOND, nc.vector.tensor_copy)
